import numpy as np
import ml_dtypes


def mxq(x, axis, fmt="e4m3"):
    dtype, down = {"e4m3": (ml_dtypes.float8_e4m3fn, 7), "e5m2": (ml_dtypes.float8_e5m2, 14)}[fmt]
    v = np.moveaxis(np.asarray(x, np.float32).astype(ml_dtypes.bfloat16).astype(np.float64), axis, -1)
    blocks = v.reshape(v.shape[:-1] + (-1, 32))
    amax = np.abs(blocks).max(-1, keepdims=True)
    byte = np.maximum(np.where(amax > 0, np.frexp(amax)[1] - 1 + 127, 0) - down, 1)
    scale = np.exp2(byte - 127.0)
    codes = (blocks / scale).astype(np.float32).astype(dtype).astype(np.float64)
    return np.moveaxis((codes * scale).reshape(v.shape), -1, axis)


WIDE = False


def mx_kscale(k):
    if not WIDE:
        return np.ones(k)
    levels = np.array([10, -10, 5, -5, 0])
    a = np.random.permutation(np.resize(levels, k // 512 * 4)).reshape(k // 512, 4)
    idx = np.arange(k)
    return np.exp2(a[idx // 512, idx % 128 // 32])


BF16 = ml_dtypes.bfloat16


def bf(x):
    return np.asarray(x, np.float32).astype(BF16)


def f64(x):
    return np.asarray(x).astype(np.float64)


E2M1 = np.array([0.0, 0.5, 1.0, 1.5, 2.0, 3.0, 4.0, 6.0, -0.0, -0.5, -1.0, -1.5, -2.0, -3.0, -4.0, -6.0])


def pack_weight(w, fmt):
    k, n = w.shape
    w = f64(bf(w)).reshape(k // 32, 32, n)
    amax = np.abs(w).max(1)
    if fmt == "e4m3":
        byte = np.frexp(amax)[1] - 1 + 127 - 7
    else:
        mant, ex = np.frexp(amax / 6.0)
        byte = np.where(mant > 0.5, ex, ex - 1) + 127
    byte = np.clip(np.where(amax > 0, byte, 1), 1, 254)
    scaled = (w * np.exp2(127.0 - byte)[:, None, :]).reshape(k, n).astype(np.float32)
    by_word = np.ascontiguousarray(scaled.reshape(k // 512, 128, 4, n).transpose(0, 1, 3, 2))
    if fmt == "e4m3":
        words = by_word.astype(ml_dtypes.float8_e4m3fn).view(np.uint8)
    else:
        c = by_word.astype(ml_dtypes.float4_e2m1fn).view(np.uint8) & 0xF
        words = c[..., 0::2] | (c[..., 1::2] << 4)
    return np.ascontiguousarray(words), np.ascontiguousarray(byte.astype(np.uint8).reshape(k // 512, 16, n))


def unpack_weight(words, scales, fmt):
    g, p, n, _ = words.shape
    if fmt == "e4m3":
        vals = np.ascontiguousarray(words).view(ml_dtypes.float8_e4m3fn).astype(np.float64)
    else:
        nib = np.empty((g, p, n, 4), np.uint8)
        nib[..., 0::2] = words & 0xF
        nib[..., 1::2] = words >> 4
        vals = E2M1[nib]
    vals = vals * np.repeat(np.exp2(scales.astype(np.float64) - 127.0), 8, axis=1)[..., None]
    return vals.transpose(0, 1, 3, 2).reshape(g * 512, n)


B, S, D = 2, 1024, 1024
EPS = 1e-8
FMT = "e4m3"


def layer_norm(v, w, b):
    mu = v.mean(-1, keepdims=True)
    var = ((v - mu) ** 2).mean(-1, keepdims=True)
    return (v - mu) / np.sqrt(var + EPS) * w + b


def setup_inputs():
    s = mx_kscale(D)
    xr = np.random.standard_normal((B, S, D)) + np.random.uniform(-1.2, 1.2, (B, S, 1))
    xi = np.random.standard_normal((B, S, D)) + np.random.uniform(-1.2, 1.2, (B, S, 1))
    words, scales = pack_weight(np.random.standard_normal((D, D)) / np.sqrt(D) / s[:, None], FMT)
    return {"x_real": bf(xr * s), "x_imag": bf(xi * s),
            "phase_matrix_words": words, "phase_matrix_scales": scales,
            "coherence_factor": bf(np.random.uniform(0.35, 0.5, 1)),
            "ln_weight": bf(1.0 + 0.1 * np.random.standard_normal(D)),
            "ln_bias": bf(0.3 * np.random.standard_normal(D))}


def reference(x_real, x_imag, phase_matrix_words, phase_matrix_scales, coherence_factor, ln_weight, ln_bias):
    xr, xi = f64(x_real), f64(x_imag)
    a, b = xr + EPS, xi + EPS
    r = np.sqrt(a * a + b * b)
    sc = (a / r).sum(-1, keepdims=True)
    ss = (b / r).sum(-1, keepdims=True)
    coherence = (sc * sc + ss * ss) / (D * D)
    p = mxq(xr, 2, "e4m3") @ unpack_weight(phase_matrix_words, phase_matrix_scales, FMT)
    p = p * f64(coherence_factor) * (1.0 - coherence)
    c, sn = np.cos(p), np.sin(p)
    new_real = xr * c - xi * sn
    new_imag = xr * sn + xi * c
    norm = np.sqrt(new_real ** 2 + new_imag ** 2 + EPS)
    new_real = new_real / norm
    new_imag = new_imag / norm
    w, bb = f64(ln_weight), f64(ln_bias)
    return (layer_norm(new_real, w, bb), layer_norm(new_imag, w, bb))

@@ -1,0 +1,270 @@
+import math
+
+import concourse.mybir as mybir
+from concourse.masks import make_identity
+
+F32 = mybir.dt.float32
+BF16 = mybir.dt.bfloat16
+I32 = mybir.dt.int32
+U32 = mybir.dt.uint32
+U8 = mybir.dt.uint8
+FP8X4 = mybir.dt.float8_e4m3fn_x4
+ALU = mybir.AluOpType
+ACT = mybir.ActivationFunctionType
+
+P = 128
+D = 1024
+TOKENS = 2048
+TILES = TOKENS // P
+K_PASS = 512
+PASSES = D // K_PASS
+BANK = 512
+HALVES = D // BANK
+LOADS_AHEAD = 3
+EPS = 1e-8
+ROUND_MAGIC = 12582912.0
+TWO_PI = 2.0 * math.pi
+
+FLOPS = 2 * TOKENS * D * D
+
+
+def tile_quantumcoherencelayer_kernel(
+    tc, x_real, x_imag, w_words, w_scale_rows, coherence_factor, ln_weight, ln_bias, out_real, out_imag
+):
+    nc = tc.nc
+    by_tile = "(p t) d -> p t d"
+    x_dram = (
+        x_real.flatten_outer_dims().rearrange(by_tile, t=TILES),
+        x_imag.flatten_outer_dims().rearrange(by_tile, t=TILES),
+    )
+    out_dram = (
+        out_real.flatten_outer_dims().rearrange(by_tile, t=TILES),
+        out_imag.flatten_outer_dims().rearrange(by_tile, t=TILES),
+    )
+
+    with tc.tile_pool(name="keep", bufs=1) as keep, tc.psum_pool(name="psum", bufs=2) as psum, tc.manual_schedule():
+        unit = keep.tile([P, TILES, 2, D], F32)
+        x_codes = keep.tile([P, TILES, PASSES, P], U32, align_bytes=64)
+        x_scales = keep.tile([P, TILES, PASSES, P], U8, align_bytes=64)
+        w_codes = keep.tile([P, PASSES, D], U32, align_bytes=64)
+        w_scales = keep.tile([P, PASSES, D], U8, align_bytes=64)
+        gain = keep.tile([P, D], BF16)
+        shift = keep.tile([P, D], BF16)
+        factor_bf = keep.tile([P, 1], BF16)
+        factor = keep.tile([P, 1], F32)
+        identity = keep.tile([P, P], F32)
+        one_col = keep.tile([P, 1], F32)
+        eps_col = keep.tile([P, 1], F32)
+        magic_col = keep.tile([P, 1], F32)
+        quarter_turn_col = keep.tile([P, 1], F32)
+        table_warmer = keep.tile([P, 1], F32)
+        minus_half = keep.tile([P, 2], F32)
+        phase_sums = keep.tile([P, 2, TILES], F32)
+        turns_per_unit = keep.tile([P, TILES], F32)
+
+        nc.vector.memset(one_col[:], 1.0)
+        nc.vector.tensor_scalar_mul(out=eps_col[:], in0=one_col[:], scalar1=EPS)
+        nc.vector.tensor_scalar_mul(out=quarter_turn_col[:], in0=one_col[:], scalar1=0.5 * math.pi)
+        nc.vector.memset(magic_col[:], ROUND_MAGIC)
+        nc.vector.memset(minus_half[:], -0.5)
+        nc.vector.memset(w_scales[:].rearrange("p g n -> p (g n)").bitcast(I32), 0)
+        make_identity(nc, identity[:])
+        nc.scalar.activation(out=table_warmer[:], in_=one_col[:], func=ACT.Abs_reciprocal_sqrt)
+
+        x_in, plain, moved, grouped = {}, {}, {}, {}
+
+        def load(i):
+            x_in[i] = stream.tile([P, 2, D], BF16, name="x_in")
+            for c in range(2):
+                nc.sync.dma_start(out=x_in[i][:, c, :], in_=x_dram[c][:, i, :])
+
+        def squares(i):
+            words = x_in[i][:, 0, :].bitcast(F32)
+            flipped = psum.tile([P, PASSES, 2, P], F32, name="flipped")
+            for g in range(PASSES):
+                for u in range(2):
+                    nc.tensor.transpose(flipped[:, g, u, :], words[:, 256 * g + u : 256 * (g + 1) : 2], identity[:])
+            plain[i] = norms.tile([P, 2, D], F32, name="plain")
+            moved[i] = norms.tile([P, 2, D], F32, name="moved")
+            nc.scalar.activation(out=plain[i][:], in_=x_in[i][:], func=ACT.Square)
+            nc.scalar.activation(out=moved[i][:], in_=x_in[i][:], func=ACT.Square, bias=eps_col[:])
+            grouped[i] = norms.tile([P, PASSES, P, 4], BF16, name="grouped", align_bytes=64)
+            nc.scalar.copy(out=grouped[i][:].bitcast(F32), in_=flipped[:].rearrange("p g u r -> p g r u"))
+
+        def add_squares(i):
+            for both in (plain[i], moved[i]):
+                nc.vector.tensor_tensor(out=both[:, 0, :], in0=both[:, 0, :], in1=both[:, 1, :], op=ALU.add)
+
+        def inverse_roots(i):
+            nc.scalar.activation(
+                out=plain[i][:, 1, :], in_=plain[i][:, 0, :], func=ACT.Abs_reciprocal_sqrt, bias=eps_col[:]
+            )
+            nc.scalar.activation(out=moved[i][:, 1, :], in_=moved[i][:, 0, :], func=ACT.Abs_reciprocal_sqrt)
+
+        def quantise(i):
+            nc.vector.quantize_mx(
+                out=x_codes[:, i].rearrange("p g r -> p (g r)").bitcast(FP8X4),
+                scales=x_scales[:, i].rearrange("p g r -> p (g r)"),
+                in_=grouped[i][:].rearrange("p g r t -> p (g r t)"),
+            )
+
+        def unit_vector(i):
+            for c in range(2):
+                nc.vector.tensor_tensor(out=unit[:, i, c, :], in0=x_in[i][:, c, :], in1=plain[i][:, 1, :], op=ALU.mult)
+
+        def coherence_sums(i):
+            for c in range(2):
+                nc.vector.scalar_tensor_tensor(
+                    out=moved[i][:, 0, :], in0=x_in[i][:, c, :], scalar=EPS, in1=moved[i][:, 1, :],
+                    op0=ALU.add, op1=ALU.mult, accum_out=phase_sums[:, c, i : i + 1],
+                )
+
+        with tc.tile_pool(name="stream", bufs=LOADS_AHEAD + 1) as stream, tc.tile_pool(name="norms", bufs=2) as norms:
+            for i in range(LOADS_AHEAD):
+                load(i)
+            squares(0)
+            for i in range(TILES):
+                add_squares(i)
+                inverse_roots(i)
+                if i + 1 < TILES:
+                    squares(i + 1)
+                quantise(i)
+                unit_vector(i)
+                coherence_sums(i)
+                if i + LOADS_AHEAD < TILES:
+                    load(i + LOADS_AHEAD)
+
+            nc.sync.dma_start(out=factor_bf[:], in_=coherence_factor.partition_broadcast(P))
+            for g in range(PASSES):
+                nc.sync.dma_start(
+                    out=w_codes[:, g, :].bitcast(I32), in_=w_words[g].rearrange("p n t -> p (n t)").bitcast(I32)
+                )
+            for quadrant in range(4):
+                nc.sync.dma_start(
+                    out=w_scales[32 * quadrant : 32 * quadrant + 4, :, :].bitcast(I32),
+                    in_=w_scale_rows[:, 4 * quadrant : 4 * quadrant + 4, :].rearrange("g r n -> r g n").bitcast(I32),
+                )
+            nc.sync.dma_start(out=gain[:], in_=ln_weight.partition_broadcast(P))
+            nc.sync.dma_start(out=shift[:], in_=ln_bias.partition_broadcast(P))
+
+            nc.vector.tensor_copy(out=factor[:], in_=factor_bf[:])
+            nc.vector.tensor_tensor(out=phase_sums[:], in0=phase_sums[:], in1=phase_sums[:], op=ALU.mult)
+            nc.vector.tensor_tensor(
+                out=turns_per_unit[:], in0=phase_sums[:, 0, :], in1=phase_sums[:, 1, :], op=ALU.add
+            )
+            nc.vector.tensor_scalar(
+                out=turns_per_unit[:], in0=turns_per_unit[:], scalar1=-1.0 / (D * D), scalar2=1.0,
+                op0=ALU.mult, op1=ALU.add,
+            )
+            nc.vector.tensor_scalar(
+                out=turns_per_unit[:], in0=turns_per_unit[:], scalar1=factor[:], scalar2=1.0 / TWO_PI,
+                op0=ALU.mult, op1=ALU.mult,
+            )
+
+        turns, rounded, cos_sin, real, total, minus_mean, spread, inv_std = {}, {}, {}, {}, {}, {}, {}, {}
+
+        def phase_in_turns(i):
+            sums = psum.tile([P, HALVES, BANK], F32, name="sums")
+            for h in range(HALVES):
+                n_cols = slice(BANK * h, BANK * (h + 1))
+                for g in range(PASSES):
+                    nc.tensor.matmul_mx(
+                        out=sums[:, h, :],
+                        lhsT=x_codes[:, i, g, :].bitcast(FP8X4),
+                        lhsT_scale=x_scales[:, i, g, :],
+                        rhs=w_codes[:, g, n_cols].bitcast(FP8X4),
+                        rhs_scale=w_scales[:, g, n_cols],
+                        start=(g == 0),
+                        stop=(g == PASSES - 1),
+                    )
+            turns[i] = angles.tile([P, HALVES, BANK], F32, name="turns")
+            for h in range(HALVES):
+                nc.scalar.activation(
+                    out=turns[i][:, h, :], in_=sums[:, h, :], func=ACT.Identity, scale=turns_per_unit[:, i : i + 1]
+                )
+            rounded[i] = angles.tile([P, HALVES, BANK], F32, name="rounded")
+            nc.scalar.activation(out=rounded[i][:], in_=turns[i][:], func=ACT.Identity, bias=magic_col[:])
+
+        def wrap(i):
+            nc.vector.scalar_tensor_tensor(
+                out=turns[i][:], in0=rounded[i][:], scalar=ROUND_MAGIC, in1=turns[i][:],
+                op0=ALU.subtract, op1=ALU.subtract,
+            )
+
+        def cos_and_sin(i):
+            flat = "p h w -> p (h w)"
+            cos_sin[i] = angles.tile([P, 2, D], F32, name="cos_sin")
+            nc.scalar.activation(out=cos_sin[i][:, 1, :], in_=turns[i][:].rearrange(flat), func=ACT.Sin, scale=-TWO_PI)
+            nc.scalar.activation(out=rounded[i][:], in_=turns[i][:], func=ACT.Abs)
+            nc.scalar.activation(
+                out=cos_sin[i][:, 0, :], in_=rounded[i][:].rearrange(flat), func=ACT.Sin, scale=-TWO_PI,
+                bias=quarter_turn_col[:],
+            )
+
+        def rotate(i):
+            a, b = unit[:, i, 0, :], unit[:, i, 1, :]
+            c, s = cos_sin[i][:, 0, :], cos_sin[i][:, 1, :]
+            real[i] = results.tile([P, 2, D], F32, name="real")
+            total[i] = small.tile([P, 2], F32, name="total")
+            nc.vector.tensor_tensor(out=real[i][:, 0, :], in0=a, in1=c, op=ALU.mult)
+            nc.vector.tensor_tensor(out=real[i][:, 1, :], in0=b, in1=s, op=ALU.mult)
+            nc.vector.scalar_tensor_tensor(
+                out=real[i][:, 0, :], in0=real[i][:, 0, :], scalar=1.0, in1=real[i][:, 1, :],
+                op0=ALU.mult, op1=ALU.subtract, accum_out=total[i][:, 0:1],
+            )
+            nc.vector.tensor_tensor(out=a, in0=a, in1=s, op=ALU.mult)
+            nc.vector.tensor_tensor(out=b, in0=b, in1=c, op=ALU.mult)
+            nc.vector.scalar_tensor_tensor(
+                out=a, in0=a, scalar=1.0, in1=b, op0=ALU.mult, op1=ALU.add, accum_out=total[i][:, 1:2]
+            )
+            minus_mean[i] = small.tile([P, 2], F32, name="minus_mean")
+            nc.gpsimd.tensor_scalar(
+                out=minus_mean[i][:], in0=total[i][:], scalar1=-1.0 / D, scalar2=0.0, op0=ALU.mult, op1=ALU.add
+            )
+
+        def rotated(i):
+            return real[i][:, 0, :], unit[:, i, 0, :]
+
+        def spreads(i):
+            unread = small.tile([P, D], BF16, name="unread", bufs=1)
+            spread[i] = small.tile([P, 2], F32, name="spread")
+            inv_std[i] = small.tile([P, 2], F32, name="inv_std")
+            for c in range(2):
+                nc.scalar.activation(
+                    out=unread[:], in_=rotated(i)[c], func=ACT.Square, bias=minus_mean[i][:, c : c + 1],
+                    accum_out=spread[i][:, c : c + 1],
+                )
+            nc.gpsimd.tensor_scalar(
+                out=spread[i][:], in0=spread[i][:], scalar1=1.0 / D, scalar2=EPS, op0=ALU.mult, op1=ALU.add
+            )
+            nc.gpsimd.tensor_tensor(out=inv_std[i][:], in0=spread[i][:], in1=minus_half[:], op=ALU.pow)
+
+        def layer_norm(i):
+            for c in range(2):
+                part = rotated(i)[c]
+                nc.vector.scalar_tensor_tensor(
+                    out=part, in0=part, scalar=minus_mean[i][:, c : c + 1], in1=gain[:], op0=ALU.add, op1=ALU.mult
+                )
+                nc.vector.scalar_tensor_tensor(
+                    out=part, in0=part, scalar=inv_std[i][:, c : c + 1], in1=shift[:], op0=ALU.mult, op1=ALU.add
+                )
+                nc.sync.dma_start(out=out_dram[c][:, i, :], in_=part)
+
+        with tc.tile_pool(name="angles", bufs=2, reuse_waits="tile") as angles, tc.tile_pool(
+            name="results", bufs=3, reuse_waits="tile"
+        ) as results, tc.tile_pool(name="small", bufs=3, reuse_waits="tile") as small:
+            phase_in_turns(0)
+            wrap(0)
+            cos_and_sin(0)
+            for i in range(TILES + 1):
+                if i + 1 < TILES:
+                    phase_in_turns(i + 1)
+                    wrap(i + 1)
+                if i >= 1:
+                    spreads(i - 1)
+                if i + 1 < TILES:
+                    cos_and_sin(i + 1)
+                if i < TILES:
+                    rotate(i)
+                if i >= 1:
+                    layer_norm(i - 1)

@@ -42,20 +42,23 @@ def tile_quantumcoherencelayer_kernel(
         out_imag.flatten_outer_dims().rearrange(by_tile, t=TILES),
     )
 
-    with tc.tile_pool(name="keep", bufs=1) as keep, tc.psum_pool(name="psum", bufs=2) as psum, tc.manual_schedule():
+    with tc.tile_pool(name="keep", bufs=1) as keep, tc.psum_pool(name="psum", bufs=2) as psum, tc.psum_pool(
+        name="vectors", bufs=1
+    ) as vectors, tc.manual_schedule():
         unit = keep.tile([P, TILES, 2, D], F32)
         x_codes = keep.tile([P, TILES, PASSES, P], U32, align_bytes=64)
         x_scales = keep.tile([P, TILES, PASSES, P], U8, align_bytes=64)
         w_codes = keep.tile([P, PASSES, D], U32, align_bytes=64)
         w_scales = keep.tile([P, PASSES, D], U8, align_bytes=64)
-        gain = keep.tile([P, D], BF16)
-        shift = keep.tile([P, D], BF16)
+        ones = keep.tile([P, P], BF16)
+        gain_shift_rows = keep.tile([P, 2, D], BF16)
         factor_bf = keep.tile([P, 1], BF16)
         factor = keep.tile([P, 1], F32)
         identity = keep.tile([P, P], F32)
         one_col = keep.tile([P, 1], F32)
         eps_col = keep.tile([P, 1], F32)
         magic_col = keep.tile([P, 1], F32)
+        minus_magic_col = keep.tile([P, 1], F32)
         quarter_turn_col = keep.tile([P, 1], F32)
         table_warmer = keep.tile([P, 1], F32)
         minus_half = keep.tile([P, 2], F32)
@@ -66,12 +69,15 @@ def tile_quantumcoherencelayer_kernel(
         nc.vector.tensor_scalar_mul(out=eps_col[:], in0=one_col[:], scalar1=EPS)
         nc.vector.tensor_scalar_mul(out=quarter_turn_col[:], in0=one_col[:], scalar1=0.5 * math.pi)
         nc.vector.memset(magic_col[:], ROUND_MAGIC)
+        nc.vector.memset(minus_magic_col[:], -ROUND_MAGIC)
+        nc.vector.memset(ones[:], 1.0)
+        nc.vector.memset(gain_shift_rows[:], 0.0)
         nc.vector.memset(minus_half[:], -0.5)
         nc.vector.memset(w_scales[:].rearrange("p g n -> p (g n)").bitcast(I32), 0)
         make_identity(nc, identity[:])
         nc.scalar.activation(out=table_warmer[:], in_=one_col[:], func=ACT.Abs_reciprocal_sqrt)
 
-        x_in, plain, moved, grouped = {}, {}, {}, {}
+        x_in, squared, grouped = {}, {}, {}
 
         def load(i):
             x_in[i] = stream.tile([P, 2, D], BF16, name="x_in")
@@ -84,22 +90,22 @@ def tile_quantumcoherencelayer_kernel(
             for g in range(PASSES):
                 for u in range(2):
                     nc.tensor.transpose(flipped[:, g, u, :], words[:, 256 * g + u : 256 * (g + 1) : 2], identity[:])
-            plain[i] = norms.tile([P, 2, D], F32, name="plain")
-            moved[i] = norms.tile([P, 2, D], F32, name="moved")
-            nc.scalar.activation(out=plain[i][:], in_=x_in[i][:], func=ACT.Square)
-            nc.scalar.activation(out=moved[i][:], in_=x_in[i][:], func=ACT.Square, bias=eps_col[:])
+            squared[i] = norms.tile([P, 2, 2, D], F32, name="squared")
+            nc.scalar.activation(out=squared[i][:, 0], in_=x_in[i][:], func=ACT.Square)
+            nc.scalar.activation(out=squared[i][:, 1], in_=x_in[i][:], func=ACT.Square, bias=eps_col[:])
             grouped[i] = norms.tile([P, PASSES, P, 4], BF16, name="grouped", align_bytes=64)
             nc.scalar.copy(out=grouped[i][:].bitcast(F32), in_=flipped[:].rearrange("p g u r -> p g r u"))
 
         def add_squares(i):
-            for both in (plain[i], moved[i]):
-                nc.vector.tensor_tensor(out=both[:, 0, :], in0=both[:, 0, :], in1=both[:, 1, :], op=ALU.add)
+            nc.vector.tensor_tensor(
+                out=squared[i][:, :, 0, :], in0=squared[i][:, :, 0, :], in1=squared[i][:, :, 1, :], op=ALU.add
+            )
 
         def inverse_roots(i):
             nc.scalar.activation(
-                out=plain[i][:, 1, :], in_=plain[i][:, 0, :], func=ACT.Abs_reciprocal_sqrt, bias=eps_col[:]
+                out=squared[i][:, 0, 1, :], in_=squared[i][:, 0, 0, :], func=ACT.Abs_reciprocal_sqrt, bias=eps_col[:]
             )
-            nc.scalar.activation(out=moved[i][:, 1, :], in_=moved[i][:, 0, :], func=ACT.Abs_reciprocal_sqrt)
+            nc.scalar.activation(out=squared[i][:, 1, 1, :], in_=squared[i][:, 1, 0, :], func=ACT.Abs_reciprocal_sqrt)
 
         def quantise(i):
             nc.vector.quantize_mx(
@@ -109,13 +115,14 @@ def tile_quantumcoherencelayer_kernel(
             )
 
         def unit_vector(i):
-            for c in range(2):
-                nc.vector.tensor_tensor(out=unit[:, i, c, :], in0=x_in[i][:, c, :], in1=plain[i][:, 1, :], op=ALU.mult)
+            nc.vector.tensor_tensor(
+                out=unit[:, i], in0=x_in[i][:], in1=squared[i][:, 0, 1:2, :].to_broadcast([P, 2, D]), op=ALU.mult
+            )
 
         def coherence_sums(i):
             for c in range(2):
                 nc.vector.scalar_tensor_tensor(
-                    out=moved[i][:, 0, :], in0=x_in[i][:, c, :], scalar=EPS, in1=moved[i][:, 1, :],
+                    out=squared[i][:, 1, 0, :], in0=x_in[i][:, c, :], scalar=EPS, in1=squared[i][:, 1, 1, :],
                     op0=ALU.add, op1=ALU.mult, accum_out=phase_sums[:, c, i : i + 1],
                 )
 
@@ -144,8 +151,16 @@ def tile_quantumcoherencelayer_kernel(
                     out=w_scales[32 * quadrant : 32 * quadrant + 4, :, :].bitcast(I32),
                     in_=w_scale_rows[:, 4 * quadrant : 4 * quadrant + 4, :].rearrange("g r n -> r g n").bitcast(I32),
                 )
-            nc.sync.dma_start(out=gain[:], in_=ln_weight.partition_broadcast(P))
-            nc.sync.dma_start(out=shift[:], in_=ln_bias.partition_broadcast(P))
+            nc.sync.dma_start(out=gain_shift_rows[0:1, 0, :], in_=ln_weight.unsqueeze(0))
+            nc.sync.dma_start(out=gain_shift_rows[0:1, 1, :], in_=ln_bias.unsqueeze(0))
+            gain = vectors.tile([P, D], BF16, name="gain")
+            shift = vectors.tile([P, D], BF16, name="shift")
+            for c, spread_out in enumerate((gain, shift)):
+                for h in range(HALVES):
+                    n_cols = slice(BANK * h, BANK * (h + 1))
+                    nc.tensor.matmul(
+                        out=spread_out[:, n_cols], lhsT=ones[:], rhs=gain_shift_rows[:, c, n_cols], start=True, stop=True
+                    )
 
             nc.vector.tensor_copy(out=factor[:], in_=factor_bf[:])
             nc.vector.tensor_tensor(out=phase_sums[:], in0=phase_sums[:], in1=phase_sums[:], op=ALU.mult)
@@ -161,15 +176,15 @@ def tile_quantumcoherencelayer_kernel(
                 op0=ALU.mult, op1=ALU.mult,
             )
 
-        turns, rounded, cos_sin, real, total, minus_mean, spread, inv_std = {}, {}, {}, {}, {}, {}, {}, {}
+        sums, rounded, turns, cos_sin, real, total, minus_mean, spread, inv_std = {}, {}, {}, {}, {}, {}, {}, {}, {}
 
-        def phase_in_turns(i):
-            sums = psum.tile([P, HALVES, BANK], F32, name="sums")
+        def whole_turns(i):
+            sums[i] = psum.tile([P, HALVES, BANK], F32, name="sums")
             for h in range(HALVES):
                 n_cols = slice(BANK * h, BANK * (h + 1))
                 for g in range(PASSES):
                     nc.tensor.matmul_mx(
-                        out=sums[:, h, :],
+                        out=sums[i][:, h, :],
                         lhsT=x_codes[:, i, g, :].bitcast(FP8X4),
                         lhsT_scale=x_scales[:, i, g, :],
                         rhs=w_codes[:, g, n_cols].bitcast(FP8X4),
@@ -177,50 +192,52 @@ def tile_quantumcoherencelayer_kernel(
                         start=(g == 0),
                         stop=(g == PASSES - 1),
                     )
-            turns[i] = angles.tile([P, HALVES, BANK], F32, name="turns")
+            rounded[i] = angles.tile([P, HALVES, BANK], F32, name="rounded")
             for h in range(HALVES):
                 nc.scalar.activation(
-                    out=turns[i][:, h, :], in_=sums[:, h, :], func=ACT.Identity, scale=turns_per_unit[:, i : i + 1]
+                    out=rounded[i][:, h, :], in_=sums[i][:, h, :], func=ACT.Identity,
+                    scale=turns_per_unit[:, i : i + 1], bias=magic_col[:],
                 )
-            rounded[i] = angles.tile([P, HALVES, BANK], F32, name="rounded")
-            nc.scalar.activation(out=rounded[i][:], in_=turns[i][:], func=ACT.Identity, bias=magic_col[:])
+            nc.scalar.activation(out=rounded[i][:], in_=rounded[i][:], func=ACT.Identity, bias=minus_magic_col[:])
 
         def wrap(i):
-            nc.vector.scalar_tensor_tensor(
-                out=turns[i][:], in0=rounded[i][:], scalar=ROUND_MAGIC, in1=turns[i][:],
-                op0=ALU.subtract, op1=ALU.subtract,
-            )
+            turns[i] = angles.tile([P, HALVES, BANK], F32, name="turns")
+            for h in range(HALVES):
+                nc.vector.scalar_tensor_tensor(
+                    out=turns[i][:, h, :], in0=sums[i][:, h, :], scalar=turns_per_unit[:, i : i + 1],
+                    in1=rounded[i][:, h, :], op0=ALU.mult, op1=ALU.subtract,
+                )
 
         def cos_and_sin(i):
             flat = "p h w -> p (h w)"
             cos_sin[i] = angles.tile([P, 2, D], F32, name="cos_sin")
-            nc.scalar.activation(out=cos_sin[i][:, 1, :], in_=turns[i][:].rearrange(flat), func=ACT.Sin, scale=-TWO_PI)
+            nc.scalar.activation(out=cos_sin[i][:, 1, :], in_=turns[i][:].rearrange(flat), func=ACT.Sin, scale=TWO_PI)
             nc.scalar.activation(out=rounded[i][:], in_=turns[i][:], func=ACT.Abs)
             nc.scalar.activation(
                 out=cos_sin[i][:, 0, :], in_=rounded[i][:].rearrange(flat), func=ACT.Sin, scale=-TWO_PI,
                 bias=quarter_turn_col[:],
             )
 
-        def rotate(i):
-            a, b = unit[:, i, 0, :], unit[:, i, 1, :]
-            c, s = cos_sin[i][:, 0, :], cos_sin[i][:, 1, :]
+        def rotate_real(i):
             real[i] = results.tile([P, 2, D], F32, name="real")
             total[i] = small.tile([P, 2], F32, name="total")
-            nc.vector.tensor_tensor(out=real[i][:, 0, :], in0=a, in1=c, op=ALU.mult)
-            nc.vector.tensor_tensor(out=real[i][:, 1, :], in0=b, in1=s, op=ALU.mult)
+            nc.vector.tensor_tensor(out=real[i][:], in0=unit[:, i], in1=cos_sin[i][:], op=ALU.mult)
             nc.vector.scalar_tensor_tensor(
                 out=real[i][:, 0, :], in0=real[i][:, 0, :], scalar=1.0, in1=real[i][:, 1, :],
                 op0=ALU.mult, op1=ALU.subtract, accum_out=total[i][:, 0:1],
             )
-            nc.vector.tensor_tensor(out=a, in0=a, in1=s, op=ALU.mult)
-            nc.vector.tensor_tensor(out=b, in0=b, in1=c, op=ALU.mult)
+
+        def cross_products(i):
+            for c in range(2):
+                nc.gpsimd.tensor_tensor(out=unit[:, i, c, :], in0=unit[:, i, c, :], in1=cos_sin[i][:, 1 - c, :], op=ALU.mult)
+
+        def rotate_imag(i):
             nc.vector.scalar_tensor_tensor(
-                out=a, in0=a, scalar=1.0, in1=b, op0=ALU.mult, op1=ALU.add, accum_out=total[i][:, 1:2]
+                out=unit[:, i, 0, :], in0=unit[:, i, 0, :], scalar=1.0, in1=unit[:, i, 1, :],
+                op0=ALU.mult, op1=ALU.add, accum_out=total[i][:, 1:2],
             )
             minus_mean[i] = small.tile([P, 2], F32, name="minus_mean")
-            nc.gpsimd.tensor_scalar(
-                out=minus_mean[i][:], in0=total[i][:], scalar1=-1.0 / D, scalar2=0.0, op0=ALU.mult, op1=ALU.add
-            )
+            nc.vector.tensor_scalar_mul(out=minus_mean[i][:], in0=total[i][:], scalar1=-1.0 / D)
 
         def rotated(i):
             return real[i][:, 0, :], unit[:, i, 0, :]
@@ -241,30 +258,36 @@ def tile_quantumcoherencelayer_kernel(
 
         def layer_norm(i):
             for c in range(2):
-                part = rotated(i)[c]
                 nc.vector.scalar_tensor_tensor(
-                    out=part, in0=part, scalar=minus_mean[i][:, c : c + 1], in1=gain[:], op0=ALU.add, op1=ALU.mult
+                    out=rotated(i)[c], in0=rotated(i)[c], scalar=minus_mean[i][:, c : c + 1], in1=gain[:],
+                    op0=ALU.add, op1=ALU.mult,
                 )
+            for c in range(2):
                 nc.vector.scalar_tensor_tensor(
-                    out=part, in0=part, scalar=inv_std[i][:, c : c + 1], in1=shift[:], op0=ALU.mult, op1=ALU.add
+                    out=rotated(i)[c], in0=rotated(i)[c], scalar=inv_std[i][:, c : c + 1], in1=shift[:],
+                    op0=ALU.mult, op1=ALU.add,
                 )
-                nc.sync.dma_start(out=out_dram[c][:, i, :], in_=part)
+                nc.sync.dma_start(out=out_dram[c][:, i, :], in_=rotated(i)[c])
 
         with tc.tile_pool(name="angles", bufs=2, reuse_waits="tile") as angles, tc.tile_pool(
             name="results", bufs=3, reuse_waits="tile"
         ) as results, tc.tile_pool(name="small", bufs=3, reuse_waits="tile") as small:
-            phase_in_turns(0)
+            whole_turns(0)
+            whole_turns(1)
             wrap(0)
             cos_and_sin(0)
             for i in range(TILES + 1):
-                if i + 1 < TILES:
-                    phase_in_turns(i + 1)
-                    wrap(i + 1)
                 if i >= 1:
                     spreads(i - 1)
-                if i + 1 < TILES:
-                    cos_and_sin(i + 1)
+                if i + 2 < TILES:
+                    whole_turns(i + 2)
                 if i < TILES:
-                    rotate(i)
+                    rotate_real(i)
+                    cross_products(i)
+                if i + 1 < TILES:
+                    wrap(i + 1)
+                    cos_and_sin(i + 1)
                 if i >= 1:
                     layer_norm(i - 1)
+                if i < TILES:
+                    rotate_imag(i)

@@ -20,7 +20,7 @@ K_PASS = 512
 PASSES = D // K_PASS
 BANK = 512
 HALVES = D // BANK
-LOADS_AHEAD = 3
+TILES_IN_WORK = 3
 EPS = 1e-8
 ROUND_MAGIC = 12582912.0
 TWO_PI = 2.0 * math.pi
@@ -93,7 +93,7 @@ def tile_quantumcoherencelayer_kernel(
             squared[i] = norms.tile([P, 2, 2, D], F32, name="squared")
             nc.scalar.activation(out=squared[i][:, 0], in_=x_in[i][:], func=ACT.Square)
             nc.scalar.activation(out=squared[i][:, 1], in_=x_in[i][:], func=ACT.Square, bias=eps_col[:])
-            grouped[i] = norms.tile([P, PASSES, P, 4], BF16, name="grouped", align_bytes=64)
+            grouped[i] = norms.tile([P, PASSES, P, 4], BF16, name="grouped", align_bytes=64, bufs=2)
             nc.scalar.copy(out=grouped[i][:].bitcast(F32), in_=flipped[:].rearrange("p g u r -> p g r u"))
 
         def add_squares(i):
@@ -126,20 +126,26 @@ def tile_quantumcoherencelayer_kernel(
                     op0=ALU.add, op1=ALU.mult, accum_out=phase_sums[:, c, i : i + 1],
                 )
 
-        with tc.tile_pool(name="stream", bufs=LOADS_AHEAD + 1) as stream, tc.tile_pool(name="norms", bufs=2) as norms:
-            for i in range(LOADS_AHEAD):
+        with tc.tile_pool(name="stream", bufs=TILES_IN_WORK + 1) as stream, tc.tile_pool(
+            name="norms", bufs=TILES_IN_WORK
+        ) as norms:
+            for i in range(TILES_IN_WORK):
                 load(i)
             squares(0)
+            squares(1)
+            add_squares(0)
+            quantise(0)
             for i in range(TILES):
-                add_squares(i)
+                if i + TILES_IN_WORK < TILES:
+                    load(i + TILES_IN_WORK)
                 inverse_roots(i)
+                if i + 2 < TILES:
+                    squares(i + 2)
                 if i + 1 < TILES:
-                    squares(i + 1)
-                quantise(i)
+                    add_squares(i + 1)
+                    quantise(i + 1)
                 unit_vector(i)
                 coherence_sums(i)
-                if i + LOADS_AHEAD < TILES:
-                    load(i + LOADS_AHEAD)
 
             nc.sync.dma_start(out=factor_bf[:], in_=coherence_factor.partition_broadcast(P))
             for g in range(PASSES):
@@ -218,20 +224,20 @@ def tile_quantumcoherencelayer_kernel(
                 bias=quarter_turn_col[:],
             )
 
-        def rotate_real(i):
+        def straight_products(i):
             real[i] = results.tile([P, 2, D], F32, name="real")
-            total[i] = small.tile([P, 2], F32, name="total")
             nc.vector.tensor_tensor(out=real[i][:], in0=unit[:, i], in1=cos_sin[i][:], op=ALU.mult)
-            nc.vector.scalar_tensor_tensor(
-                out=real[i][:, 0, :], in0=real[i][:, 0, :], scalar=1.0, in1=real[i][:, 1, :],
-                op0=ALU.mult, op1=ALU.subtract, accum_out=total[i][:, 0:1],
-            )
 
         def cross_products(i):
             for c in range(2):
                 nc.gpsimd.tensor_tensor(out=unit[:, i, c, :], in0=unit[:, i, c, :], in1=cos_sin[i][:, 1 - c, :], op=ALU.mult)
 
-        def rotate_imag(i):
+        def combine(i):
+            total[i] = small.tile([P, 2], F32, name="total")
+            nc.vector.scalar_tensor_tensor(
+                out=real[i][:, 0, :], in0=real[i][:, 0, :], scalar=1.0, in1=real[i][:, 1, :],
+                op0=ALU.mult, op1=ALU.subtract, accum_out=total[i][:, 0:1],
+            )
             nc.vector.scalar_tensor_tensor(
                 out=unit[:, i, 0, :], in0=unit[:, i, 0, :], scalar=1.0, in1=unit[:, i, 1, :],
                 op0=ALU.mult, op1=ALU.add, accum_out=total[i][:, 1:2],
@@ -282,7 +288,7 @@ def tile_quantumcoherencelayer_kernel(
                 if i + 2 < TILES:
                     whole_turns(i + 2)
                 if i < TILES:
-                    rotate_real(i)
+                    straight_products(i)
                     cross_products(i)
                 if i + 1 < TILES:
                     wrap(i + 1)
@@ -290,4 +296,4 @@ def tile_quantumcoherencelayer_kernel(
                 if i >= 1:
                     layer_norm(i - 1)
                 if i < TILES:
-                    rotate_imag(i)
+                    combine(i)

@@ -276,24 +276,24 @@ def tile_quantumcoherencelayer_kernel(
                 nc.sync.dma_start(out=out_dram[c][:, i, :], in_=rotated(i)[c])
 
         with tc.tile_pool(name="angles", bufs=2, reuse_waits="tile") as angles, tc.tile_pool(
-            name="results", bufs=3, reuse_waits="tile"
-        ) as results, tc.tile_pool(name="small", bufs=3, reuse_waits="tile") as small:
+            name="results", bufs=4, reuse_waits="tile"
+        ) as results, tc.tile_pool(name="small", bufs=4, reuse_waits="tile") as small:
             whole_turns(0)
             whole_turns(1)
             wrap(0)
             cos_and_sin(0)
-            for i in range(TILES + 1):
-                if i >= 1:
-                    spreads(i - 1)
-                if i + 2 < TILES:
-                    whole_turns(i + 2)
+            for i in range(TILES + 2):
                 if i < TILES:
                     straight_products(i)
                     cross_products(i)
+                if 1 <= i <= TILES:
+                    spreads(i - 1)
+                if i + 2 < TILES:
+                    whole_turns(i + 2)
                 if i + 1 < TILES:
                     wrap(i + 1)
                     cos_and_sin(i + 1)
-                if i >= 1:
-                    layer_norm(i - 1)
+                if i >= 2:
+                    layer_norm(i - 2)
                 if i < TILES:
                     combine(i)

@@ -16,10 +16,14 @@ P = 128
 D = 1024
 TOKENS = 2048
 TILES = TOKENS // P
-K_PASS = 512
+PACK = 4
+K_PASS = P * PACK
 PASSES = D // K_PASS
+PAIRS_PER_PASS = K_PASS // 2
 BANK = 512
 HALVES = D // BANK
+QUADRANT = 32
+SCALE_ROWS = 4
 TILES_IN_WORK = 3
 EPS = 1e-8
 ROUND_MAGIC = 12582912.0
@@ -70,9 +74,9 @@ def tile_quantumcoherencelayer_kernel(
         nc.vector.tensor_scalar_mul(out=quarter_turn_col[:], in0=one_col[:], scalar1=0.5 * math.pi)
         nc.vector.memset(magic_col[:], ROUND_MAGIC)
         nc.vector.memset(minus_magic_col[:], -ROUND_MAGIC)
+        nc.vector.memset(minus_half[:], -0.5)
         nc.vector.memset(ones[:], 1.0)
         nc.vector.memset(gain_shift_rows[:], 0.0)
-        nc.vector.memset(minus_half[:], -0.5)
         nc.vector.memset(w_scales[:].rearrange("p g n -> p (g n)").bitcast(I32), 0)
         make_identity(nc, identity[:])
         nc.scalar.activation(out=table_warmer[:], in_=one_col[:], func=ACT.Abs_reciprocal_sqrt)
@@ -81,31 +85,29 @@ def tile_quantumcoherencelayer_kernel(
 
         def load(i):
             x_in[i] = stream.tile([P, 2, D], BF16, name="x_in")
-            for c in range(2):
-                nc.sync.dma_start(out=x_in[i][:, c, :], in_=x_dram[c][:, i, :])
+            for part in range(2):
+                nc.sync.dma_start(out=x_in[i][:, part, :], in_=x_dram[part][:, i, :])
 
         def squares(i):
-            words = x_in[i][:, 0, :].bitcast(F32)
+            pairs = x_in[i][:, 0, :].bitcast(F32)
             flipped = psum.tile([P, PASSES, 2, P], F32, name="flipped")
             for g in range(PASSES):
                 for u in range(2):
-                    nc.tensor.transpose(flipped[:, g, u, :], words[:, 256 * g + u : 256 * (g + 1) : 2], identity[:])
+                    nc.tensor.transpose(
+                        flipped[:, g, u, :],
+                        pairs[:, PAIRS_PER_PASS * g + u : PAIRS_PER_PASS * (g + 1) : 2],
+                        identity[:],
+                    )
             squared[i] = norms.tile([P, 2, 2, D], F32, name="squared")
             nc.scalar.activation(out=squared[i][:, 0], in_=x_in[i][:], func=ACT.Square)
             nc.scalar.activation(out=squared[i][:, 1], in_=x_in[i][:], func=ACT.Square, bias=eps_col[:])
-            grouped[i] = norms.tile([P, PASSES, P, 4], BF16, name="grouped", align_bytes=64, bufs=2)
+            grouped[i] = norms.tile([P, PASSES, P, PACK], BF16, name="grouped", align_bytes=64, bufs=2)
             nc.scalar.copy(out=grouped[i][:].bitcast(F32), in_=flipped[:].rearrange("p g u r -> p g r u"))
 
         def add_squares(i):
             nc.vector.tensor_tensor(
                 out=squared[i][:, :, 0, :], in0=squared[i][:, :, 0, :], in1=squared[i][:, :, 1, :], op=ALU.add
             )
-
-        def inverse_roots(i):
-            nc.scalar.activation(
-                out=squared[i][:, 0, 1, :], in_=squared[i][:, 0, 0, :], func=ACT.Abs_reciprocal_sqrt, bias=eps_col[:]
-            )
-            nc.scalar.activation(out=squared[i][:, 1, 1, :], in_=squared[i][:, 1, 0, :], func=ACT.Abs_reciprocal_sqrt)
 
         def quantise(i):
             nc.vector.quantize_mx(
@@ -114,16 +116,22 @@ def tile_quantumcoherencelayer_kernel(
                 in_=grouped[i][:].rearrange("p g r t -> p (g r t)"),
             )
 
+        def inverse_roots(i):
+            nc.scalar.activation(
+                out=squared[i][:, 0, 1, :], in_=squared[i][:, 0, 0, :], func=ACT.Abs_reciprocal_sqrt, bias=eps_col[:]
+            )
+            nc.scalar.activation(out=squared[i][:, 1, 1, :], in_=squared[i][:, 1, 0, :], func=ACT.Abs_reciprocal_sqrt)
+
         def unit_vector(i):
             nc.vector.tensor_tensor(
                 out=unit[:, i], in0=x_in[i][:], in1=squared[i][:, 0, 1:2, :].to_broadcast([P, 2, D]), op=ALU.mult
             )
 
         def coherence_sums(i):
-            for c in range(2):
+            for part in range(2):
                 nc.vector.scalar_tensor_tensor(
-                    out=squared[i][:, 1, 0, :], in0=x_in[i][:, c, :], scalar=EPS, in1=squared[i][:, 1, 1, :],
-                    op0=ALU.add, op1=ALU.mult, accum_out=phase_sums[:, c, i : i + 1],
+                    out=squared[i][:, 1, 0, :], in0=x_in[i][:, part, :], scalar=EPS, in1=squared[i][:, 1, 1, :],
+                    op0=ALU.add, op1=ALU.mult, accum_out=phase_sums[:, part, i : i + 1],
                 )
 
         with tc.tile_pool(name="stream", bufs=TILES_IN_WORK + 1) as stream, tc.tile_pool(
@@ -152,20 +160,21 @@ def tile_quantumcoherencelayer_kernel(
                 nc.sync.dma_start(
                     out=w_codes[:, g, :].bitcast(I32), in_=w_words[g].rearrange("p n t -> p (n t)").bitcast(I32)
                 )
-            for quadrant in range(4):
+            for quadrant in range(P // QUADRANT):
+                rows = slice(SCALE_ROWS * quadrant, SCALE_ROWS * (quadrant + 1))
                 nc.sync.dma_start(
-                    out=w_scales[32 * quadrant : 32 * quadrant + 4, :, :].bitcast(I32),
-                    in_=w_scale_rows[:, 4 * quadrant : 4 * quadrant + 4, :].rearrange("g r n -> r g n").bitcast(I32),
+                    out=w_scales[QUADRANT * quadrant : QUADRANT * quadrant + SCALE_ROWS, :, :].bitcast(I32),
+                    in_=w_scale_rows[:, rows, :].rearrange("g r n -> r g n").bitcast(I32),
                 )
             nc.sync.dma_start(out=gain_shift_rows[0:1, 0, :], in_=ln_weight.unsqueeze(0))
             nc.sync.dma_start(out=gain_shift_rows[0:1, 1, :], in_=ln_bias.unsqueeze(0))
             gain = vectors.tile([P, D], BF16, name="gain")
             shift = vectors.tile([P, D], BF16, name="shift")
-            for c, spread_out in enumerate((gain, shift)):
+            for row, repeated in enumerate((gain, shift)):
                 for h in range(HALVES):
                     n_cols = slice(BANK * h, BANK * (h + 1))
                     nc.tensor.matmul(
-                        out=spread_out[:, n_cols], lhsT=ones[:], rhs=gain_shift_rows[:, c, n_cols], start=True, stop=True
+                        out=repeated[:, n_cols], lhsT=ones[:], rhs=gain_shift_rows[:, row, n_cols], start=True, stop=True
                     )
 
             nc.vector.tensor_copy(out=factor[:], in_=factor_bf[:])
@@ -229,8 +238,10 @@ def tile_quantumcoherencelayer_kernel(
             nc.vector.tensor_tensor(out=real[i][:], in0=unit[:, i], in1=cos_sin[i][:], op=ALU.mult)
 
         def cross_products(i):
-            for c in range(2):
-                nc.gpsimd.tensor_tensor(out=unit[:, i, c, :], in0=unit[:, i, c, :], in1=cos_sin[i][:, 1 - c, :], op=ALU.mult)
+            for part in range(2):
+                nc.gpsimd.tensor_tensor(
+                    out=unit[:, i, part, :], in0=unit[:, i, part, :], in1=cos_sin[i][:, 1 - part, :], op=ALU.mult
+                )
 
         def combine(i):
             total[i] = small.tile([P, 2], F32, name="total")
@@ -252,10 +263,10 @@ def tile_quantumcoherencelayer_kernel(
             unread = small.tile([P, D], BF16, name="unread", bufs=1)
             spread[i] = small.tile([P, 2], F32, name="spread")
             inv_std[i] = small.tile([P, 2], F32, name="inv_std")
-            for c in range(2):
+            for part in range(2):
                 nc.scalar.activation(
-                    out=unread[:], in_=rotated(i)[c], func=ACT.Square, bias=minus_mean[i][:, c : c + 1],
-                    accum_out=spread[i][:, c : c + 1],
+                    out=unread[:], in_=rotated(i)[part], func=ACT.Square, bias=minus_mean[i][:, part : part + 1],
+                    accum_out=spread[i][:, part : part + 1],
                 )
             nc.gpsimd.tensor_scalar(
                 out=spread[i][:], in0=spread[i][:], scalar1=1.0 / D, scalar2=EPS, op0=ALU.mult, op1=ALU.add
@@ -263,25 +274,26 @@ def tile_quantumcoherencelayer_kernel(
             nc.gpsimd.tensor_tensor(out=inv_std[i][:], in0=spread[i][:], in1=minus_half[:], op=ALU.pow)
 
         def layer_norm(i):
-            for c in range(2):
+            for part in range(2):
                 nc.vector.scalar_tensor_tensor(
-                    out=rotated(i)[c], in0=rotated(i)[c], scalar=minus_mean[i][:, c : c + 1], in1=gain[:],
+                    out=rotated(i)[part], in0=rotated(i)[part], scalar=minus_mean[i][:, part : part + 1], in1=gain[:],
                     op0=ALU.add, op1=ALU.mult,
                 )
-            for c in range(2):
+            for part in range(2):
                 nc.vector.scalar_tensor_tensor(
-                    out=rotated(i)[c], in0=rotated(i)[c], scalar=inv_std[i][:, c : c + 1], in1=shift[:],
+                    out=rotated(i)[part], in0=rotated(i)[part], scalar=inv_std[i][:, part : part + 1], in1=shift[:],
                     op0=ALU.mult, op1=ALU.add,
                 )
-                nc.sync.dma_start(out=out_dram[c][:, i, :], in_=rotated(i)[c])
+                nc.sync.dma_start(out=out_dram[part][:, i, :], in_=rotated(i)[part])
 
         with tc.tile_pool(name="angles", bufs=2, reuse_waits="tile") as angles, tc.tile_pool(
             name="results", bufs=4, reuse_waits="tile"
         ) as results, tc.tile_pool(name="small", bufs=4, reuse_waits="tile") as small:
             whole_turns(0)
-            whole_turns(1)
             wrap(0)
+            nc.scalar.activation(out=table_warmer[:], in_=one_col[:], func=ACT.Sin)
             cos_and_sin(0)
+            whole_turns(1)
             for i in range(TILES + 2):
                 if i < TILES:
                     straight_products(i)

@@ -24,7 +24,8 @@ BANK = 512
 HALVES = D // BANK
 QUADRANT = 32
 SCALE_ROWS = 4
-TILES_IN_WORK = 3
+BLOCKS = BANK // P
+UNITS = 2 * HALVES
 EPS = 1e-8
 ROUND_MAGIC = 12582912.0
 TWO_PI = 2.0 * math.pi
@@ -46,9 +47,7 @@ def tile_quantumcoherencelayer_kernel(
         out_imag.flatten_outer_dims().rearrange(by_tile, t=TILES),
     )
 
-    with tc.tile_pool(name="keep", bufs=1) as keep, tc.psum_pool(name="psum", bufs=2) as psum, tc.psum_pool(
-        name="vectors", bufs=1
-    ) as vectors, tc.manual_schedule():
+    with tc.tile_pool(name="keep", bufs=1) as keep, tc.manual_schedule():
         unit = keep.tile([P, TILES, 2, D], F32)
         x_codes = keep.tile([P, TILES, PASSES, P], U32, align_bytes=64)
         x_scales = keep.tile([P, TILES, PASSES, P], U8, align_bytes=64)
@@ -66,7 +65,7 @@ def tile_quantumcoherencelayer_kernel(
         quarter_turn_col = keep.tile([P, 1], F32)
         table_warmer = keep.tile([P, 1], F32)
         minus_half = keep.tile([P, 2], F32)
-        phase_sums = keep.tile([P, 2, TILES], F32)
+        phase_sums = keep.tile([P, 2, HALVES, TILES], F32)
         turns_per_unit = keep.tile([P, TILES], F32)
 
         nc.vector.memset(one_col[:], 1.0)
@@ -81,32 +80,42 @@ def tile_quantumcoherencelayer_kernel(
         make_identity(nc, identity[:])
         nc.scalar.activation(out=table_warmer[:], in_=one_col[:], func=ACT.Abs_reciprocal_sqrt)
 
-        x_in, squared, grouped = {}, {}, {}
+        x_in, squared, linear, grouped, folded, inverse_t, unfolded = {}, {}, {}, {}, {}, {}, {}
 
         def load(i):
             x_in[i] = stream.tile([P, 2, D], BF16, name="x_in")
             for part in range(2):
                 nc.sync.dma_start(out=x_in[i][:, part, :], in_=x_dram[part][:, i, :])
 
-        def squares(i):
+        def flip(i):
             pairs = x_in[i][:, 0, :].bitcast(F32)
-            flipped = psum.tile([P, PASSES, 2, P], F32, name="flipped")
+            flipped[i] = psum1.tile([P, PASSES, 2, P], F32, name="flipped", bufs=2)
             for g in range(PASSES):
                 for u in range(2):
                     nc.tensor.transpose(
-                        flipped[:, g, u, :],
+                        flipped[i][:, g, u, :],
                         pairs[:, PAIRS_PER_PASS * g + u : PAIRS_PER_PASS * (g + 1) : 2],
                         identity[:],
                     )
-            squared[i] = norms.tile([P, 2, 2, D], F32, name="squared")
-            nc.scalar.activation(out=squared[i][:, 0], in_=x_in[i][:], func=ACT.Square)
-            nc.scalar.activation(out=squared[i][:, 1], in_=x_in[i][:], func=ACT.Square, bias=eps_col[:])
-            grouped[i] = norms.tile([P, PASSES, P, PACK], BF16, name="grouped", align_bytes=64, bufs=2)
-            nc.scalar.copy(out=grouped[i][:].bitcast(F32), in_=flipped[:].rearrange("p g u r -> p g r u"))
 
-        def add_squares(i):
-            nc.vector.tensor_tensor(
-                out=squared[i][:, :, 0, :], in0=squared[i][:, :, 0, :], in1=squared[i][:, :, 1, :], op=ALU.add
+        def group(i):
+            grouped[i] = work.tile([P, PASSES, P, PACK], BF16, name="grouped", align_bytes=64, bufs=2)
+            nc.scalar.copy(out=grouped[i][:].bitcast(F32), in_=flipped[i][:].rearrange("p g u r -> p g r u"))
+
+        def square(i, piece):
+            if piece == 0:
+                squared[i] = work.tile([P, 2, D], F32, name="squared")
+            cols = slice(D // UNITS * piece, D // UNITS * (piece + 1))
+            nc.scalar.activation(out=squared[i][:, :, cols], in_=x_in[i][:, :, cols], func=ACT.Square)
+
+        def add_parts(i):
+            linear[i] = work.tile([P, D], F32, name="linear")
+            nc.gpsimd.tensor_tensor(out=linear[i][:], in0=x_in[i][:, 0, :], in1=x_in[i][:, 1, :], op=ALU.add)
+
+        def scale_parts(i):
+            nc.gpsimd.tensor_scalar(
+                out=linear[i][:], in0=linear[i][:], scalar1=2.0 * EPS, scalar2=2.0 * EPS * EPS,
+                op0=ALU.mult, op1=ALU.add,
             )
 
         def quantise(i):
@@ -116,44 +125,86 @@ def tile_quantumcoherencelayer_kernel(
                 in_=grouped[i][:].rearrange("p g r t -> p (g r t)"),
             )
 
-        def inverse_roots(i):
-            nc.scalar.activation(
-                out=squared[i][:, 0, 1, :], in_=squared[i][:, 0, 0, :], func=ACT.Abs_reciprocal_sqrt, bias=eps_col[:]
-            )
-            nc.scalar.activation(out=squared[i][:, 1, 1, :], in_=squared[i][:, 1, 0, :], func=ACT.Abs_reciprocal_sqrt)
+        def unit_of(n):
+            return n // UNITS, (n % UNITS) // 2, n % 2 == 1
 
-        def unit_vector(i):
-            nc.vector.tensor_tensor(
-                out=unit[:, i], in0=x_in[i][:], in1=squared[i][:, 0, 1:2, :].to_broadcast([P, 2, D]), op=ALU.mult
-            )
+        def fold(n):
+            i, h, shifted = unit_of(n)
+            folded[n] = psum1.tile([P, BANK], F32, name="folded")
+            terms = [squared[i][:, 0, :], squared[i][:, 1, :]] + ([linear[i][:]] if shifted else [])
+            for block in range(BLOCKS):
+                cols = slice(BANK * h + P * block, BANK * h + P * (block + 1))
+                for t, term in enumerate(terms):
+                    nc.tensor.matmul(
+                        out=folded[n][:, P * block : P * (block + 1)], lhsT=term[:, cols], rhs=identity[:],
+                        is_transpose=True, start=(t == 0), stop=(t == len(terms) - 1),
+                    )
 
-        def coherence_sums(i):
-            for part in range(2):
-                nc.vector.scalar_tensor_tensor(
-                    out=squared[i][:, 1, 0, :], in0=x_in[i][:, part, :], scalar=EPS, in1=squared[i][:, 1, 1, :],
-                    op0=ALU.add, op1=ALU.mult, accum_out=phase_sums[:, part, i : i + 1],
+        def roots(n):
+            i, h, shifted = unit_of(n)
+            inverse_t[n] = work.tile([P, BANK], F32, name="inverse_t", bufs=4)
+            if shifted:
+                nc.scalar.activation(out=inverse_t[n][:], in_=folded[n][:], func=ACT.Abs_reciprocal_sqrt)
+            else:
+                nc.scalar.activation(
+                    out=inverse_t[n][:], in_=folded[n][:], func=ACT.Abs_reciprocal_sqrt, bias=eps_col[:]
                 )
 
-        with tc.tile_pool(name="stream", bufs=TILES_IN_WORK + 1) as stream, tc.tile_pool(
-            name="norms", bufs=TILES_IN_WORK
-        ) as norms:
-            for i in range(TILES_IN_WORK):
+        def unfold(n):
+            unfolded[n] = psum1.tile([P, 1, BANK], F32, name="unfolded")
+            for block in range(BLOCKS):
+                cols = slice(P * block, P * (block + 1))
+                nc.tensor.transpose(unfolded[n][:, 0, cols], inverse_t[n][:, cols], identity[:])
+
+        def products(n):
+            i, h, shifted = unit_of(n)
+            cols = slice(BANK * h, BANK * (h + 1))
+            if shifted:
+                unread = work.tile([P, BANK], BF16, name="unread", bufs=1)
+                for part in range(2):
+                    nc.vector.scalar_tensor_tensor(
+                        out=unread[:], in0=x_in[i][:, part, cols], scalar=EPS, in1=unfolded[n][:, 0, :],
+                        op0=ALU.add, op1=ALU.mult, accum_out=phase_sums[:, part, h, i : i + 1],
+                    )
+            else:
+                nc.vector.tensor_tensor(
+                    out=unit[:, i, :, cols], in0=x_in[i][:, :, cols],
+                    in1=unfolded[n][:].to_broadcast([P, 2, BANK]), op=ALU.mult,
+                )
+
+        def prepare(i, step):
+            square(i, step)
+            if step == 0:
+                add_parts(i)
+                flip(i)
+            if step == 1:
+                scale_parts(i)
+                group(i)
+            if step == 2:
+                quantise(i)
+
+        flipped = {}
+        with tc.tile_pool(name="stream", bufs=4) as stream, tc.tile_pool(name="work", bufs=3) as work, tc.psum_pool(
+            name="psum1", bufs=3
+        ) as psum1:
+            for i in range(3):
                 load(i)
-            squares(0)
-            squares(1)
-            add_squares(0)
-            quantise(0)
-            for i in range(TILES):
-                if i + TILES_IN_WORK < TILES:
-                    load(i + TILES_IN_WORK)
-                inverse_roots(i)
-                if i + 2 < TILES:
-                    squares(i + 2)
+            for step in range(UNITS):
+                prepare(0, step)
+            for n in range(UNITS * TILES + 3):
+                i, step = n // UNITS, n % UNITS
+                if n < UNITS * TILES:
+                    fold(n)
+                if 1 <= n <= UNITS * TILES:
+                    roots(n - 1)
                 if i + 1 < TILES:
-                    add_squares(i + 1)
-                    quantise(i + 1)
-                unit_vector(i)
-                coherence_sums(i)
+                    prepare(i + 1, step)
+                if 2 <= n <= UNITS * TILES + 1:
+                    unfold(n - 2)
+                if n >= 3:
+                    products(n - 3)
+                if step == 3 and i + 3 < TILES:
+                    load(i + 3)
 
             nc.sync.dma_start(out=factor_bf[:], in_=coherence_factor.partition_broadcast(P))
             for g in range(PASSES):
@@ -168,28 +219,6 @@ def tile_quantumcoherencelayer_kernel(
                 )
             nc.sync.dma_start(out=gain_shift_rows[0:1, 0, :], in_=ln_weight.unsqueeze(0))
             nc.sync.dma_start(out=gain_shift_rows[0:1, 1, :], in_=ln_bias.unsqueeze(0))
-            gain = vectors.tile([P, D], BF16, name="gain")
-            shift = vectors.tile([P, D], BF16, name="shift")
-            for row, repeated in enumerate((gain, shift)):
-                for h in range(HALVES):
-                    n_cols = slice(BANK * h, BANK * (h + 1))
-                    nc.tensor.matmul(
-                        out=repeated[:, n_cols], lhsT=ones[:], rhs=gain_shift_rows[:, row, n_cols], start=True, stop=True
-                    )
-
-            nc.vector.tensor_copy(out=factor[:], in_=factor_bf[:])
-            nc.vector.tensor_tensor(out=phase_sums[:], in0=phase_sums[:], in1=phase_sums[:], op=ALU.mult)
-            nc.vector.tensor_tensor(
-                out=turns_per_unit[:], in0=phase_sums[:, 0, :], in1=phase_sums[:, 1, :], op=ALU.add
-            )
-            nc.vector.tensor_scalar(
-                out=turns_per_unit[:], in0=turns_per_unit[:], scalar1=-1.0 / (D * D), scalar2=1.0,
-                op0=ALU.mult, op1=ALU.add,
-            )
-            nc.vector.tensor_scalar(
-                out=turns_per_unit[:], in0=turns_per_unit[:], scalar1=factor[:], scalar2=1.0 / TWO_PI,
-                op0=ALU.mult, op1=ALU.mult,
-            )
 
         sums, rounded, turns, cos_sin, real, total, minus_mean, spread, inv_std = {}, {}, {}, {}, {}, {}, {}, {}, {}
 
@@ -286,9 +315,36 @@ def tile_quantumcoherencelayer_kernel(
                 )
                 nc.sync.dma_start(out=out_dram[part][:, i, :], in_=rotated(i)[part])
 
-        with tc.tile_pool(name="angles", bufs=2, reuse_waits="tile") as angles, tc.tile_pool(
-            name="results", bufs=4, reuse_waits="tile"
-        ) as results, tc.tile_pool(name="small", bufs=4, reuse_waits="tile") as small:
+        with tc.psum_pool(name="psum", bufs=2) as psum, tc.psum_pool(name="vectors", bufs=1) as vectors, tc.tile_pool(
+            name="angles", bufs=2, reuse_waits="tile"
+        ) as angles, tc.tile_pool(name="results", bufs=4, reuse_waits="tile") as results, tc.tile_pool(
+            name="small", bufs=4, reuse_waits="tile"
+        ) as small:
+            gain = vectors.tile([P, D], BF16, name="gain")
+            shift = vectors.tile([P, D], BF16, name="shift")
+            for row, repeated in enumerate((gain, shift)):
+                for h in range(HALVES):
+                    n_cols = slice(BANK * h, BANK * (h + 1))
+                    nc.tensor.matmul(
+                        out=repeated[:, n_cols], lhsT=ones[:], rhs=gain_shift_rows[:, row, n_cols], start=True, stop=True
+                    )
+
+            nc.vector.tensor_copy(out=factor[:], in_=factor_bf[:])
+            whole_sums = phase_sums[:, :, 0, :]
+            nc.vector.tensor_tensor(out=whole_sums, in0=whole_sums, in1=phase_sums[:, :, 1, :], op=ALU.add)
+            nc.vector.tensor_tensor(out=whole_sums, in0=whole_sums, in1=whole_sums, op=ALU.mult)
+            nc.vector.tensor_tensor(
+                out=turns_per_unit[:], in0=phase_sums[:, 0, 0, :], in1=phase_sums[:, 1, 0, :], op=ALU.add
+            )
+            nc.vector.tensor_scalar(
+                out=turns_per_unit[:], in0=turns_per_unit[:], scalar1=-1.0 / (D * D), scalar2=1.0,
+                op0=ALU.mult, op1=ALU.add,
+            )
+            nc.vector.tensor_scalar(
+                out=turns_per_unit[:], in0=turns_per_unit[:], scalar1=factor[:], scalar2=1.0 / TWO_PI,
+                op0=ALU.mult, op1=ALU.mult,
+            )
+
             whole_turns(0)
             wrap(0)
             nc.scalar.activation(out=table_warmer[:], in_=one_col[:], func=ACT.Sin)

@@ -108,14 +108,10 @@ def tile_quantumcoherencelayer_kernel(
             cols = slice(D // UNITS * piece, D // UNITS * (piece + 1))
             nc.scalar.activation(out=squared[i][:, :, cols], in_=x_in[i][:, :, cols], func=ACT.Square)
 
-        def add_parts(i):
-            linear[i] = work.tile([P, D], F32, name="linear")
-            nc.gpsimd.tensor_tensor(out=linear[i][:], in0=x_in[i][:, 0, :], in1=x_in[i][:, 1, :], op=ALU.add)
-
-        def scale_parts(i):
+        def linear_terms(i):
+            linear[i] = work.tile([P, 2, D], F32, name="linear", bufs=2)
             nc.gpsimd.tensor_scalar(
-                out=linear[i][:], in0=linear[i][:], scalar1=2.0 * EPS, scalar2=2.0 * EPS * EPS,
-                op0=ALU.mult, op1=ALU.add,
+                out=linear[i][:], in0=x_in[i][:], scalar1=2.0 * EPS, scalar2=EPS * EPS, op0=ALU.mult, op1=ALU.add
             )
 
         def quantise(i):
@@ -131,7 +127,9 @@ def tile_quantumcoherencelayer_kernel(
         def fold(n):
             i, h, shifted = unit_of(n)
             folded[n] = psum1.tile([P, BANK], F32, name="folded")
-            terms = [squared[i][:, 0, :], squared[i][:, 1, :]] + ([linear[i][:]] if shifted else [])
+            terms = [squared[i][:, 0, :], squared[i][:, 1, :]]
+            if shifted:
+                terms = terms + [linear[i][:, 0, :], linear[i][:, 1, :]]
             for block in range(BLOCKS):
                 cols = slice(BANK * h + P * block, BANK * h + P * (block + 1))
                 for t, term in enumerate(terms):
@@ -175,10 +173,9 @@ def tile_quantumcoherencelayer_kernel(
         def prepare(i, step):
             square(i, step)
             if step == 0:
-                add_parts(i)
+                linear_terms(i)
                 flip(i)
             if step == 1:
-                scale_parts(i)
                 group(i)
             if step == 2:
                 quantise(i)

@@ -114,6 +114,9 @@ def tile_quantumcoherencelayer_kernel(
                 out=linear[i][:], in0=x_in[i][:], scalar1=2.0 * EPS, scalar2=EPS * EPS, op0=ALU.mult, op1=ALU.add
             )
 
+        def add_linear_terms(i):
+            nc.gpsimd.tensor_tensor(out=linear[i][:, 0, :], in0=linear[i][:, 0, :], in1=linear[i][:, 1, :], op=ALU.add)
+
         def quantise(i):
             nc.vector.quantize_mx(
                 out=x_codes[:, i].rearrange("p g r -> p (g r)").bitcast(FP8X4),
@@ -129,7 +132,7 @@ def tile_quantumcoherencelayer_kernel(
             folded[n] = psum1.tile([P, BANK], F32, name="folded")
             terms = [squared[i][:, 0, :], squared[i][:, 1, :]]
             if shifted:
-                terms = terms + [linear[i][:, 0, :], linear[i][:, 1, :]]
+                terms = terms + [linear[i][:, 0, :]]
             for block in range(BLOCKS):
                 cols = slice(BANK * h + P * block, BANK * h + P * (block + 1))
                 for t, term in enumerate(terms):
@@ -176,8 +179,9 @@ def tile_quantumcoherencelayer_kernel(
                 linear_terms(i)
                 flip(i)
             if step == 1:
+                add_linear_terms(i)
                 group(i)
-            if step == 2:
+            if step == 3:
                 quantise(i)
 
         flipped = {}

@@ -67,6 +67,7 @@ def tile_quantumcoherencelayer_kernel(
         minus_half = keep.tile([P, 2], F32)
         phase_sums = keep.tile([P, 2, HALVES, TILES], F32)
         turns_per_unit = keep.tile([P, TILES], F32)
+        gain_rows = keep.tile([P, D], BF16)
 
         nc.vector.memset(one_col[:], 1.0)
         nc.vector.tensor_scalar_mul(out=eps_col[:], in0=one_col[:], scalar1=EPS)
@@ -114,9 +115,6 @@ def tile_quantumcoherencelayer_kernel(
                 out=linear[i][:], in0=x_in[i][:], scalar1=2.0 * EPS, scalar2=EPS * EPS, op0=ALU.mult, op1=ALU.add
             )
 
-        def add_linear_terms(i):
-            nc.gpsimd.tensor_tensor(out=linear[i][:, 0, :], in0=linear[i][:, 0, :], in1=linear[i][:, 1, :], op=ALU.add)
-
         def quantise(i):
             nc.vector.quantize_mx(
                 out=x_codes[:, i].rearrange("p g r -> p (g r)").bitcast(FP8X4),
@@ -132,7 +130,7 @@ def tile_quantumcoherencelayer_kernel(
             folded[n] = psum1.tile([P, BANK], F32, name="folded")
             terms = [squared[i][:, 0, :], squared[i][:, 1, :]]
             if shifted:
-                terms = terms + [linear[i][:, 0, :]]
+                terms = terms + [linear[i][:, 0, :], linear[i][:, 1, :]]
             for block in range(BLOCKS):
                 cols = slice(BANK * h + P * block, BANK * h + P * (block + 1))
                 for t, term in enumerate(terms):
@@ -179,9 +177,8 @@ def tile_quantumcoherencelayer_kernel(
                 linear_terms(i)
                 flip(i)
             if step == 1:
-                add_linear_terms(i)
                 group(i)
-            if step == 3:
+            if step == 2:
                 quantise(i)
 
         flipped = {}
@@ -222,8 +219,9 @@ def tile_quantumcoherencelayer_kernel(
             nc.sync.dma_start(out=gain_shift_rows[0:1, 1, :], in_=ln_bias.unsqueeze(0))
 
         sums, rounded, turns, cos_sin, real, total, minus_mean, spread, inv_std = {}, {}, {}, {}, {}, {}, {}, {}, {}
+        real_t, real_t_rows, real_back = {}, {}, {}
 
-        def whole_turns(i):
+        def multiply(i):
             sums[i] = psum.tile([P, HALVES, BANK], F32, name="sums")
             for h in range(HALVES):
                 n_cols = slice(BANK * h, BANK * (h + 1))
@@ -237,6 +235,8 @@ def tile_quantumcoherencelayer_kernel(
                         start=(g == 0),
                         stop=(g == PASSES - 1),
                     )
+
+        def whole_turns(i):
             rounded[i] = angles.tile([P, HALVES, BANK], F32, name="rounded")
             for h in range(HALVES):
                 nc.scalar.activation(
@@ -257,15 +257,47 @@ def tile_quantumcoherencelayer_kernel(
             flat = "p h w -> p (h w)"
             cos_sin[i] = angles.tile([P, 2, D], F32, name="cos_sin")
             nc.scalar.activation(out=cos_sin[i][:, 1, :], in_=turns[i][:].rearrange(flat), func=ACT.Sin, scale=TWO_PI)
-            nc.scalar.activation(out=rounded[i][:], in_=turns[i][:], func=ACT.Abs)
+            nc.scalar.activation(out=cos_sin[i][:, 0, :], in_=turns[i][:].rearrange(flat), func=ACT.Abs)
             nc.scalar.activation(
-                out=cos_sin[i][:, 0, :], in_=rounded[i][:].rearrange(flat), func=ACT.Sin, scale=-TWO_PI,
-                bias=quarter_turn_col[:],
+                out=cos_sin[i][:, 0, :], in_=cos_sin[i][:, 0, :], func=ACT.Sin, scale=-TWO_PI, bias=quarter_turn_col[:]
             )
 
         def straight_products(i):
             real[i] = results.tile([P, 2, D], F32, name="real")
-            nc.vector.tensor_tensor(out=real[i][:], in0=unit[:, i], in1=cos_sin[i][:], op=ALU.mult)
+            total[i] = small.tile([P, 3], F32, name="total")
+            minus_mean[i] = small.tile([P, 2], F32, name="minus_mean")
+            for part, sign in enumerate((1.0, -1.0)):
+                nc.vector.scalar_tensor_tensor(
+                    out=real[i][:, part, :], in0=unit[:, i, part, :], scalar=sign, in1=cos_sin[i][:, part, :],
+                    op0=ALU.mult, op1=ALU.mult, accum_out=total[i][:, part : part + 1],
+                )
+            nc.vector.tensor_scalar(
+                out=minus_mean[i][:, 0:1], in0=total[i][:, 0:1], scalar1=total[i][:, 1:2], scalar2=-1.0 / D,
+                op0=ALU.add, op1=ALU.mult,
+            )
+
+        def fold_real(i):
+            real_t[i] = psum.tile([P, HALVES, BANK], F32, name="real_t")
+            for h in range(HALVES):
+                for block in range(BLOCKS):
+                    cols = slice(BANK * h + P * block, BANK * h + P * (block + 1))
+                    for part in range(2):
+                        nc.tensor.matmul(
+                            out=real_t[i][:, h, P * block : P * (block + 1)], lhsT=real[i][:, part, cols],
+                            rhs=identity[:], is_transpose=True, start=(part == 0), stop=(part == 1),
+                        )
+
+        def evacuate(i):
+            real_t_rows[i] = turned.tile([P, HALVES, BANK], F32, name="real_t_rows")
+            for h in range(HALVES):
+                nc.scalar.copy(out=real_t_rows[i][:, h, :], in_=real_t[i][:, h, :])
+
+        def unfold_real(i):
+            real_back[i] = psum.tile([P, HALVES, BANK], F32, name="real_back")
+            for h in range(HALVES):
+                for block in range(BLOCKS):
+                    cols = slice(P * block, P * (block + 1))
+                    nc.tensor.transpose(real_back[i][:, h, cols], real_t_rows[i][:, h, cols], identity[:])
 
         def cross_products(i):
             for part in range(2):
@@ -273,62 +305,68 @@ def tile_quantumcoherencelayer_kernel(
                     out=unit[:, i, part, :], in0=unit[:, i, part, :], in1=cos_sin[i][:, 1 - part, :], op=ALU.mult
                 )
 
-        def combine(i):
-            total[i] = small.tile([P, 2], F32, name="total")
-            nc.vector.scalar_tensor_tensor(
-                out=real[i][:, 0, :], in0=real[i][:, 0, :], scalar=1.0, in1=real[i][:, 1, :],
-                op0=ALU.mult, op1=ALU.subtract, accum_out=total[i][:, 0:1],
-            )
+        def combine_imag(i):
             nc.vector.scalar_tensor_tensor(
                 out=unit[:, i, 0, :], in0=unit[:, i, 0, :], scalar=1.0, in1=unit[:, i, 1, :],
-                op0=ALU.mult, op1=ALU.add, accum_out=total[i][:, 1:2],
+                op0=ALU.mult, op1=ALU.add, accum_out=total[i][:, 2:3],
             )
-            minus_mean[i] = small.tile([P, 2], F32, name="minus_mean")
-            nc.vector.tensor_scalar_mul(out=minus_mean[i][:], in0=total[i][:], scalar1=-1.0 / D)
-
-        def rotated(i):
-            return real[i][:, 0, :], unit[:, i, 0, :]
+            nc.vector.tensor_scalar_mul(out=minus_mean[i][:, 1:2], in0=total[i][:, 2:3], scalar1=-1.0 / D)
 
         def spreads(i):
             unread = small.tile([P, D], BF16, name="unread", bufs=1)
-            spread[i] = small.tile([P, 2], F32, name="spread")
-            inv_std[i] = small.tile([P, 2], F32, name="inv_std")
-            for part in range(2):
-                nc.scalar.activation(
-                    out=unread[:], in_=rotated(i)[part], func=ACT.Square, bias=minus_mean[i][:, part : part + 1],
-                    accum_out=spread[i][:, part : part + 1],
-                )
-            nc.gpsimd.tensor_scalar(
-                out=spread[i][:], in0=spread[i][:], scalar1=1.0 / D, scalar2=EPS, op0=ALU.mult, op1=ALU.add
+            spread[i] = small.tile([P, 3], F32, name="spread")
+            nc.scalar.activation(
+                out=unread[:], in_=unit[:, i, 0, :], func=ACT.Square, bias=minus_mean[i][:, 1:2],
+                accum_out=spread[i][:, 2:3],
             )
-            nc.gpsimd.tensor_tensor(out=inv_std[i][:], in0=spread[i][:], in1=minus_half[:], op=ALU.pow)
-
-        def layer_norm(i):
-            for part in range(2):
-                nc.vector.scalar_tensor_tensor(
-                    out=rotated(i)[part], in0=rotated(i)[part], scalar=minus_mean[i][:, part : part + 1], in1=gain[:],
-                    op0=ALU.add, op1=ALU.mult,
+            for h in range(HALVES):
+                nc.scalar.activation(
+                    out=unread[:, 0:BANK], in_=real_back[i][:, h, :], func=ACT.Square, bias=minus_mean[i][:, 0:1],
+                    accum_out=spread[i][:, h : h + 1],
                 )
-            for part in range(2):
+
+        def deviations(i):
+            inv_std[i] = small.tile([P, 2], F32, name="inv_std")
+            nc.gpsimd.tensor_tensor(out=spread[i][:, 1:2], in0=spread[i][:, 0:1], in1=spread[i][:, 1:2], op=ALU.add)
+            nc.gpsimd.tensor_scalar(
+                out=spread[i][:, 1:3], in0=spread[i][:, 1:3], scalar1=1.0 / D, scalar2=EPS, op0=ALU.mult, op1=ALU.add
+            )
+            nc.gpsimd.tensor_tensor(out=inv_std[i][:], in0=spread[i][:, 1:3], in1=minus_half[:], op=ALU.pow)
+
+        def layer_norm_first(i):
+            for h in range(HALVES):
+                cols = slice(BANK * h, BANK * (h + 1))
                 nc.vector.scalar_tensor_tensor(
-                    out=rotated(i)[part], in0=rotated(i)[part], scalar=inv_std[i][:, part : part + 1], in1=shift[:],
+                    out=real[i][:, 0, cols], in0=real_back[i][:, h, :], scalar=minus_mean[i][:, 0:1],
+                    in1=gain_rows[:, cols], op0=ALU.add, op1=ALU.mult,
+                )
+            nc.vector.scalar_tensor_tensor(
+                out=unit[:, i, 0, :], in0=unit[:, i, 0, :], scalar=minus_mean[i][:, 1:2], in1=gain[:],
+                op0=ALU.add, op1=ALU.mult,
+            )
+
+        def layer_norm_second(i):
+            for part, values in enumerate((real[i][:, 0, :], unit[:, i, 0, :])):
+                nc.vector.scalar_tensor_tensor(
+                    out=values, in0=values, scalar=inv_std[i][:, part : part + 1], in1=shift[:],
                     op0=ALU.mult, op1=ALU.add,
                 )
-                nc.sync.dma_start(out=out_dram[part][:, i, :], in_=rotated(i)[part])
+                nc.sync.dma_start(out=out_dram[part][:, i, :], in_=values)
 
-        with tc.psum_pool(name="psum", bufs=2) as psum, tc.psum_pool(name="vectors", bufs=1) as vectors, tc.tile_pool(
+        with tc.psum_pool(name="psum", bufs=1) as psum, tc.tile_pool(
             name="angles", bufs=2, reuse_waits="tile"
         ) as angles, tc.tile_pool(name="results", bufs=4, reuse_waits="tile") as results, tc.tile_pool(
             name="small", bufs=4, reuse_waits="tile"
-        ) as small:
-            gain = vectors.tile([P, D], BF16, name="gain")
-            shift = vectors.tile([P, D], BF16, name="shift")
+        ) as small, tc.tile_pool(name="turned", bufs=1) as turned:
+            gain = psum.tile([P, D], BF16, name="gain")
+            shift = psum.tile([P, D], BF16, name="shift")
             for row, repeated in enumerate((gain, shift)):
                 for h in range(HALVES):
                     n_cols = slice(BANK * h, BANK * (h + 1))
                     nc.tensor.matmul(
                         out=repeated[:, n_cols], lhsT=ones[:], rhs=gain_shift_rows[:, row, n_cols], start=True, stop=True
                     )
+            nc.scalar.copy(out=gain_rows[:], in_=gain[:])
 
             nc.vector.tensor_copy(out=factor[:], in_=factor_bf[:])
             whole_sums = phase_sums[:, :, 0, :]
@@ -346,23 +384,34 @@ def tile_quantumcoherencelayer_kernel(
                 op0=ALU.mult, op1=ALU.mult,
             )
 
+            multiply(0)
             whole_turns(0)
-            wrap(0)
             nc.scalar.activation(out=table_warmer[:], in_=one_col[:], func=ACT.Sin)
-            cos_and_sin(0)
-            whole_turns(1)
-            for i in range(TILES + 2):
-                if i < TILES:
+            for i in range(-2, TILES + 2):
+                here = 0 <= i < TILES
+                if here:
                     straight_products(i)
-                    cross_products(i)
+                    fold_real(i)
+                if i + 2 < TILES:
+                    wrap(i + 2)
+                if i + 3 < TILES:
+                    multiply(i + 3)
                 if 1 <= i <= TILES:
                     spreads(i - 1)
-                if i + 2 < TILES:
-                    whole_turns(i + 2)
-                if i + 1 < TILES:
-                    wrap(i + 1)
+                if here:
+                    cross_products(i)
+                if 1 <= i <= TILES:
+                    deviations(i - 1)
+                if 0 <= i + 1 < TILES:
                     cos_and_sin(i + 1)
+                if 1 <= i <= TILES:
+                    layer_norm_first(i - 1)
                 if i >= 2:
-                    layer_norm(i - 2)
-                if i < TILES:
-                    combine(i)
+                    layer_norm_second(i - 2)
+                if here:
+                    evacuate(i)
+                    unfold_real(i)
+                if i + 3 < TILES:
+                    whole_turns(i + 3)
+                if here:
+                    combine_imag(i)

@@ -271,10 +271,6 @@ def tile_quantumcoherencelayer_kernel(
                     out=real[i][:, part, :], in0=unit[:, i, part, :], scalar=sign, in1=cos_sin[i][:, part, :],
                     op0=ALU.mult, op1=ALU.mult, accum_out=total[i][:, part : part + 1],
                 )
-            nc.vector.tensor_scalar(
-                out=minus_mean[i][:, 0:1], in0=total[i][:, 0:1], scalar1=total[i][:, 1:2], scalar2=-1.0 / D,
-                op0=ALU.add, op1=ALU.mult,
-            )
 
         def fold_real(i):
             real_t[i] = psum.tile([P, HALVES, BANK], F32, name="real_t")
@@ -311,6 +307,10 @@ def tile_quantumcoherencelayer_kernel(
                 op0=ALU.mult, op1=ALU.add, accum_out=total[i][:, 2:3],
             )
             nc.vector.tensor_scalar_mul(out=minus_mean[i][:, 1:2], in0=total[i][:, 2:3], scalar1=-1.0 / D)
+            nc.vector.tensor_scalar(
+                out=minus_mean[i][:, 0:1], in0=total[i][:, 0:1], scalar1=total[i][:, 1:2], scalar2=-1.0 / D,
+                op0=ALU.add, op1=ALU.mult,
+            )
 
         def spreads(i):
             unread = small.tile([P, D], BF16, name="unread", bufs=1)

@@ -358,6 +358,7 @@ def tile_quantumcoherencelayer_kernel(
         ) as angles, tc.tile_pool(name="results", bufs=4, reuse_waits="tile") as results, tc.tile_pool(
             name="small", bufs=4, reuse_waits="tile"
         ) as small, tc.tile_pool(name="turned", bufs=1) as turned:
+            multiply(0)
             gain = psum.tile([P, D], BF16, name="gain")
             shift = psum.tile([P, D], BF16, name="shift")
             for row, repeated in enumerate((gain, shift)):
@@ -366,7 +367,6 @@ def tile_quantumcoherencelayer_kernel(
                     nc.tensor.matmul(
                         out=repeated[:, n_cols], lhsT=ones[:], rhs=gain_shift_rows[:, row, n_cols], start=True, stop=True
                     )
-            nc.scalar.copy(out=gain_rows[:], in_=gain[:])
 
             nc.vector.tensor_copy(out=factor[:], in_=factor_bf[:])
             whole_sums = phase_sums[:, :, 0, :]
@@ -384,9 +384,9 @@ def tile_quantumcoherencelayer_kernel(
                 op0=ALU.mult, op1=ALU.mult,
             )
 
-            multiply(0)
             whole_turns(0)
             nc.scalar.activation(out=table_warmer[:], in_=one_col[:], func=ACT.Sin)
+            nc.vector.tensor_copy(out=gain_rows[:], in_=gain[:])
             for i in range(-2, TILES + 2):
                 here = 0 <= i < TILES
                 if here:

@@ -68,6 +68,7 @@ def tile_quantumcoherencelayer_kernel(
         phase_sums = keep.tile([P, 2, HALVES, TILES], F32)
         turns_per_unit = keep.tile([P, TILES], F32)
         gain_rows = keep.tile([P, D], BF16)
+        spare = keep.tile([P, 2, D], F32)
 
         nc.vector.memset(one_col[:], 1.0)
         nc.vector.tensor_scalar_mul(out=eps_col[:], in0=one_col[:], scalar1=EPS)
@@ -141,7 +142,7 @@ def tile_quantumcoherencelayer_kernel(
 
         def roots(n):
             i, h, shifted = unit_of(n)
-            inverse_t[n] = work.tile([P, BANK], F32, name="inverse_t", bufs=4)
+            inverse_t[n] = work.tile([P, BANK], F32, name="inverse_t")
             if shifted:
                 nc.scalar.activation(out=inverse_t[n][:], in_=folded[n][:], func=ACT.Abs_reciprocal_sqrt)
             else:
@@ -159,10 +160,9 @@ def tile_quantumcoherencelayer_kernel(
             i, h, shifted = unit_of(n)
             cols = slice(BANK * h, BANK * (h + 1))
             if shifted:
-                unread = work.tile([P, BANK], BF16, name="unread", bufs=1)
                 for part in range(2):
                     nc.vector.scalar_tensor_tensor(
-                        out=unread[:], in0=x_in[i][:, part, cols], scalar=EPS, in1=unfolded[n][:, 0, :],
+                        out=gain_rows[:, 0:BANK], in0=x_in[i][:, part, cols], scalar=EPS, in1=unfolded[n][:, 0, :],
                         op0=ALU.add, op1=ALU.mult, accum_out=phase_sums[:, part, h, i : i + 1],
                     )
             else:
@@ -181,53 +181,16 @@ def tile_quantumcoherencelayer_kernel(
             if step == 2:
                 quantise(i)
 
-        flipped = {}
-        with tc.tile_pool(name="stream", bufs=4) as stream, tc.tile_pool(name="work", bufs=3) as work, tc.psum_pool(
-            name="psum1", bufs=3
-        ) as psum1:
-            for i in range(3):
-                load(i)
-            for step in range(UNITS):
-                prepare(0, step)
-            for n in range(UNITS * TILES + 3):
-                i, step = n // UNITS, n % UNITS
-                if n < UNITS * TILES:
-                    fold(n)
-                if 1 <= n <= UNITS * TILES:
-                    roots(n - 1)
-                if i + 1 < TILES:
-                    prepare(i + 1, step)
-                if 2 <= n <= UNITS * TILES + 1:
-                    unfold(n - 2)
-                if n >= 3:
-                    products(n - 3)
-                if step == 3 and i + 3 < TILES:
-                    load(i + 3)
-
-            nc.sync.dma_start(out=factor_bf[:], in_=coherence_factor.partition_broadcast(P))
-            for g in range(PASSES):
-                nc.sync.dma_start(
-                    out=w_codes[:, g, :].bitcast(I32), in_=w_words[g].rearrange("p n t -> p (n t)").bitcast(I32)
-                )
-            for quadrant in range(P // QUADRANT):
-                rows = slice(SCALE_ROWS * quadrant, SCALE_ROWS * (quadrant + 1))
-                nc.sync.dma_start(
-                    out=w_scales[QUADRANT * quadrant : QUADRANT * quadrant + SCALE_ROWS, :, :].bitcast(I32),
-                    in_=w_scale_rows[:, rows, :].rearrange("g r n -> r g n").bitcast(I32),
-                )
-            nc.sync.dma_start(out=gain_shift_rows[0:1, 0, :], in_=ln_weight.unsqueeze(0))
-            nc.sync.dma_start(out=gain_shift_rows[0:1, 1, :], in_=ln_bias.unsqueeze(0))
-
         sums, rounded, turns, cos_sin, real, total, minus_mean, spread, inv_std = {}, {}, {}, {}, {}, {}, {}, {}, {}
         real_t, real_t_rows, real_back = {}, {}, {}
 
-        def multiply(i):
-            sums[i] = psum.tile([P, HALVES, BANK], F32, name="sums")
+        def multiply(i, banks):
+            sums[i] = banks
             for h in range(HALVES):
                 n_cols = slice(BANK * h, BANK * (h + 1))
                 for g in range(PASSES):
                     nc.tensor.matmul_mx(
-                        out=sums[i][:, h, :],
+                        out=sums[i][h],
                         lhsT=x_codes[:, i, g, :].bitcast(FP8X4),
                         lhsT_scale=x_scales[:, i, g, :],
                         rhs=w_codes[:, g, n_cols].bitcast(FP8X4),
@@ -236,26 +199,34 @@ def tile_quantumcoherencelayer_kernel(
                         stop=(g == PASSES - 1),
                     )
 
+        def sums_banks():
+            both = psum.tile([P, HALVES, BANK], F32, name="sums")
+            return [both[:, h, :] for h in range(HALVES)]
+
+        def add_magic(i, h):
+            nc.scalar.activation(
+                out=rounded[i][:, h, :], in_=sums[i][h], func=ACT.Identity,
+                scale=turns_per_unit[:, i : i + 1], bias=magic_col[:],
+            )
+
+        def take_magic_away(i):
+            nc.scalar.activation(out=rounded[i][:], in_=rounded[i][:], func=ACT.Identity, bias=minus_magic_col[:])
+
         def whole_turns(i):
             rounded[i] = angles.tile([P, HALVES, BANK], F32, name="rounded")
             for h in range(HALVES):
-                nc.scalar.activation(
-                    out=rounded[i][:, h, :], in_=sums[i][:, h, :], func=ACT.Identity,
-                    scale=turns_per_unit[:, i : i + 1], bias=magic_col[:],
-                )
-            nc.scalar.activation(out=rounded[i][:], in_=rounded[i][:], func=ACT.Identity, bias=minus_magic_col[:])
+                add_magic(i, h)
+            take_magic_away(i)
 
         def wrap(i):
-            turns[i] = angles.tile([P, HALVES, BANK], F32, name="turns")
             for h in range(HALVES):
                 nc.vector.scalar_tensor_tensor(
-                    out=turns[i][:, h, :], in0=sums[i][:, h, :], scalar=turns_per_unit[:, i : i + 1],
+                    out=turns[i][:, h, :], in0=sums[i][h], scalar=turns_per_unit[:, i : i + 1],
                     in1=rounded[i][:, h, :], op0=ALU.mult, op1=ALU.subtract,
                 )
 
         def cos_and_sin(i):
             flat = "p h w -> p (h w)"
-            cos_sin[i] = angles.tile([P, 2, D], F32, name="cos_sin")
             nc.scalar.activation(out=cos_sin[i][:, 1, :], in_=turns[i][:].rearrange(flat), func=ACT.Sin, scale=TWO_PI)
             nc.scalar.activation(out=cos_sin[i][:, 0, :], in_=turns[i][:].rearrange(flat), func=ACT.Abs)
             nc.scalar.activation(
@@ -263,7 +234,7 @@ def tile_quantumcoherencelayer_kernel(
             )
 
         def straight_products(i):
-            real[i] = results.tile([P, 2, D], F32, name="real")
+            real[i] = spare if i % 4 == 3 else results.tile([P, 2, D], F32, name="real")
             total[i] = small.tile([P, 3], F32, name="total")
             minus_mean[i] = small.tile([P, 2], F32, name="minus_mean")
             for part, sign in enumerate((1.0, -1.0)):
@@ -353,12 +324,89 @@ def tile_quantumcoherencelayer_kernel(
                 )
                 nc.sync.dma_start(out=out_dram[part][:, i, :], in_=values)
 
+        def turns_of(tiles):
+            whole_sums = phase_sums[:, :, 0, tiles]
+            nc.vector.tensor_tensor(out=whole_sums, in0=whole_sums, in1=phase_sums[:, :, 1, tiles], op=ALU.add)
+            nc.vector.tensor_tensor(out=whole_sums, in0=whole_sums, in1=whole_sums, op=ALU.mult)
+            nc.vector.tensor_tensor(
+                out=turns_per_unit[:, tiles], in0=phase_sums[:, 0, 0, tiles], in1=phase_sums[:, 1, 0, tiles], op=ALU.add
+            )
+            nc.vector.tensor_scalar(
+                out=turns_per_unit[:, tiles], in0=turns_per_unit[:, tiles], scalar1=-1.0 / (D * D), scalar2=1.0,
+                op0=ALU.mult, op1=ALU.add,
+            )
+            nc.vector.tensor_scalar(
+                out=turns_per_unit[:, tiles], in0=turns_per_unit[:, tiles], scalar1=factor[:], scalar2=1.0 / TWO_PI,
+                op0=ALU.mult, op1=ALU.mult,
+            )
+
+        def load_the_rest():
+            nc.sync.dma_start(out=factor_bf[:], in_=coherence_factor.partition_broadcast(P))
+            for g in range(PASSES):
+                nc.sync.dma_start(
+                    out=w_codes[:, g, :].bitcast(I32), in_=w_words[g].rearrange("p n t -> p (n t)").bitcast(I32)
+                )
+            for quadrant in range(P // QUADRANT):
+                rows = slice(SCALE_ROWS * quadrant, SCALE_ROWS * (quadrant + 1))
+                nc.sync.dma_start(
+                    out=w_scales[QUADRANT * quadrant : QUADRANT * quadrant + SCALE_ROWS, :, :].bitcast(I32),
+                    in_=w_scale_rows[:, rows, :].rearrange("g r n -> r g n").bitcast(I32),
+                )
+            nc.sync.dma_start(out=gain_shift_rows[0:1, 0, :], in_=ln_weight.unsqueeze(0))
+            nc.sync.dma_start(out=gain_shift_rows[0:1, 1, :], in_=ln_bias.unsqueeze(0))
+
+        flipped = {}
+        EARLY_TILES = 12
+        last = UNITS * TILES - 1
+        with tc.tile_pool(name="stream", bufs=4) as stream, tc.tile_pool(name="work", bufs=3) as work, tc.psum_pool(
+            name="psum1", bufs=3
+        ) as psum1:
+            for i in range(3):
+                load(i)
+            for step in range(UNITS):
+                prepare(0, step)
+            for n in range(UNITS * TILES + 3):
+                i, step = n // UNITS, n % UNITS
+                if n < UNITS * TILES:
+                    fold(n)
+                if 1 <= n <= UNITS * TILES:
+                    roots(n - 1)
+                if i + 1 < TILES:
+                    prepare(i + 1, step)
+                if 2 <= n <= UNITS * TILES + 1:
+                    unfold(n - 2)
+                if n >= 3:
+                    products(n - 3)
+                if step == 3 and i + 3 < TILES:
+                    load(i + 3)
+                if n == 11:
+                    load_the_rest()
+                if n == UNITS * (EARLY_TILES + 1) + 2:
+                    nc.vector.tensor_copy(out=factor[:], in_=factor_bf[:])
+                    turns_of(slice(0, EARLY_TILES))
+                if n == last - 3:
+                    multiply(0, [psum1.tile([P, BANK], F32, name="flipped", bufs=2)[:] for h in range(HALVES)])
+                if n == last - 2:
+                    rounded[0] = work.tile([P, HALVES, BANK], F32, name="linear", bufs=2)
+                    add_magic(0, 0)
+                if n == last - 1:
+                    add_magic(0, 1)
+                if n == last:
+                    take_magic_away(0)
+                if n == last + 1:
+                    nc.scalar.activation(out=table_warmer[:], in_=one_col[:], func=ACT.Sin)
+                    turns[0] = work.tile([P, HALVES, BANK], F32, name="linear", bufs=2)
+                    wrap(0)
+                if n == last + 2:
+                    cos_sin[0] = spare
+                    cos_and_sin(0)
+
         with tc.psum_pool(name="psum", bufs=1) as psum, tc.tile_pool(
             name="angles", bufs=2, reuse_waits="tile"
-        ) as angles, tc.tile_pool(name="results", bufs=4, reuse_waits="tile") as results, tc.tile_pool(
+        ) as angles, tc.tile_pool(name="results", bufs=3, reuse_waits="tile") as results, tc.tile_pool(
             name="small", bufs=4, reuse_waits="tile"
         ) as small, tc.tile_pool(name="turned", bufs=1) as turned:
-            multiply(0)
+            multiply(1, sums_banks())
             gain = psum.tile([P, D], BF16, name="gain")
             shift = psum.tile([P, D], BF16, name="shift")
             for row, repeated in enumerate((gain, shift)):
@@ -367,42 +415,27 @@ def tile_quantumcoherencelayer_kernel(
                     nc.tensor.matmul(
                         out=repeated[:, n_cols], lhsT=ones[:], rhs=gain_shift_rows[:, row, n_cols], start=True, stop=True
                     )
-
-            nc.vector.tensor_copy(out=factor[:], in_=factor_bf[:])
-            whole_sums = phase_sums[:, :, 0, :]
-            nc.vector.tensor_tensor(out=whole_sums, in0=whole_sums, in1=phase_sums[:, :, 1, :], op=ALU.add)
-            nc.vector.tensor_tensor(out=whole_sums, in0=whole_sums, in1=whole_sums, op=ALU.mult)
-            nc.vector.tensor_tensor(
-                out=turns_per_unit[:], in0=phase_sums[:, 0, 0, :], in1=phase_sums[:, 1, 0, :], op=ALU.add
-            )
-            nc.vector.tensor_scalar(
-                out=turns_per_unit[:], in0=turns_per_unit[:], scalar1=-1.0 / (D * D), scalar2=1.0,
-                op0=ALU.mult, op1=ALU.add,
-            )
-            nc.vector.tensor_scalar(
-                out=turns_per_unit[:], in0=turns_per_unit[:], scalar1=factor[:], scalar2=1.0 / TWO_PI,
-                op0=ALU.mult, op1=ALU.mult,
-            )
-
-            whole_turns(0)
-            nc.scalar.activation(out=table_warmer[:], in_=one_col[:], func=ACT.Sin)
+            turns_of(slice(EARLY_TILES, TILES))
             nc.vector.tensor_copy(out=gain_rows[:], in_=gain[:])
+
             for i in range(-2, TILES + 2):
                 here = 0 <= i < TILES
                 if here:
                     straight_products(i)
                     fold_real(i)
-                if i + 2 < TILES:
+                if 1 <= i + 2 < TILES:
+                    turns[i + 2] = angles.tile([P, HALVES, BANK], F32, name="turns")
                     wrap(i + 2)
-                if i + 3 < TILES:
-                    multiply(i + 3)
+                if 2 <= i + 3 < TILES:
+                    multiply(i + 3, sums_banks())
                 if 1 <= i <= TILES:
                     spreads(i - 1)
                 if here:
                     cross_products(i)
                 if 1 <= i <= TILES:
                     deviations(i - 1)
-                if 0 <= i + 1 < TILES:
+                if 1 <= i + 1 < TILES:
+                    cos_sin[i + 1] = angles.tile([P, 2, D], F32, name="cos_sin")
                     cos_and_sin(i + 1)
                 if 1 <= i <= TILES:
                     layer_norm_first(i - 1)

@@ -162,7 +162,7 @@ def tile_quantumcoherencelayer_kernel(
             if shifted:
                 for part in range(2):
                     nc.vector.scalar_tensor_tensor(
-                        out=gain_rows[:, 0:BANK], in0=x_in[i][:, part, cols], scalar=EPS, in1=unfolded[n][:, 0, :],
+                        out=gain_rows[:, BANK * part : BANK * (part + 1)], in0=x_in[i][:, part, cols], scalar=EPS, in1=unfolded[n][:, 0, :],
                         op0=ALU.add, op1=ALU.mult, accum_out=phase_sums[:, part, h, i : i + 1],
                     )
             else:
@@ -209,16 +209,21 @@ def tile_quantumcoherencelayer_kernel(
                 scale=turns_per_unit[:, i : i + 1], bias=magic_col[:],
             )
 
-        def take_magic_away(i):
-            nc.scalar.activation(out=rounded[i][:], in_=rounded[i][:], func=ACT.Identity, bias=minus_magic_col[:])
+        def take_magic_away(i, h):
+            nc.scalar.activation(
+                out=rounded[i][:, h, :], in_=rounded[i][:, h, :], func=ACT.Identity, bias=minus_magic_col[:]
+            )
 
-        def whole_turns(i):
-            rounded[i] = angles.tile([P, HALVES, BANK], F32, name="rounded")
+        def whole_turns_on_vector(i):
+            rounded[i] = angles.tile([P, HALVES, BANK], I32, name="rounded")
             for h in range(HALVES):
-                add_magic(i, h)
-            take_magic_away(i)
+                nc.vector.tensor_scalar_mul(
+                    out=rounded[i][:, h, :], in0=sums[i][h], scalar1=turns_per_unit[:, i : i + 1]
+                )
 
         def wrap(i):
+            if i in ROUNDED_ON_VECTOR:
+                whole_turns_on_vector(i)
             for h in range(HALVES):
                 nc.vector.scalar_tensor_tensor(
                     out=turns[i][:, h, :], in0=sums[i][h], scalar=turns_per_unit[:, i : i + 1],
@@ -227,8 +232,8 @@ def tile_quantumcoherencelayer_kernel(
 
         def cos_and_sin(i):
             flat = "p h w -> p (h w)"
-            nc.scalar.activation(out=cos_sin[i][:, 1, :], in_=turns[i][:].rearrange(flat), func=ACT.Sin, scale=TWO_PI)
             nc.scalar.activation(out=cos_sin[i][:, 0, :], in_=turns[i][:].rearrange(flat), func=ACT.Abs)
+            nc.scalar.activation(out=cos_sin[i][:, 1, :], in_=turns[i][:].rearrange(flat), func=ACT.Sin, scale=TWO_PI)
             nc.scalar.activation(
                 out=cos_sin[i][:, 0, :], in_=cos_sin[i][:, 0, :], func=ACT.Sin, scale=-TWO_PI, bias=quarter_turn_col[:]
             )
@@ -254,10 +259,10 @@ def tile_quantumcoherencelayer_kernel(
                             rhs=identity[:], is_transpose=True, start=(part == 0), stop=(part == 1),
                         )
 
-        def evacuate(i):
-            real_t_rows[i] = turned.tile([P, HALVES, BANK], F32, name="real_t_rows")
-            for h in range(HALVES):
-                nc.scalar.copy(out=real_t_rows[i][:, h, :], in_=real_t[i][:, h, :])
+        def evacuate(i, h):
+            if h == 0:
+                real_t_rows[i] = turned.tile([P, HALVES, BANK], F32, name="real_t_rows")
+            nc.scalar.copy(out=real_t_rows[i][:, h, :], in_=real_t[i][:, h, :])
 
         def unfold_real(i):
             real_back[i] = psum.tile([P, HALVES, BANK], F32, name="real_back")
@@ -277,22 +282,22 @@ def tile_quantumcoherencelayer_kernel(
                 out=unit[:, i, 0, :], in0=unit[:, i, 0, :], scalar=1.0, in1=unit[:, i, 1, :],
                 op0=ALU.mult, op1=ALU.add, accum_out=total[i][:, 2:3],
             )
-            nc.vector.tensor_scalar_mul(out=minus_mean[i][:, 1:2], in0=total[i][:, 2:3], scalar1=-1.0 / D)
             nc.vector.tensor_scalar(
                 out=minus_mean[i][:, 0:1], in0=total[i][:, 0:1], scalar1=total[i][:, 1:2], scalar2=-1.0 / D,
                 op0=ALU.add, op1=ALU.mult,
             )
+            nc.vector.tensor_scalar_mul(out=minus_mean[i][:, 1:2], in0=total[i][:, 2:3], scalar1=-1.0 / D)
 
         def spreads(i):
-            unread = small.tile([P, D], BF16, name="unread", bufs=1)
+            unread = small.tile([P, 2 * D], BF16, name="unread", bufs=1)
             spread[i] = small.tile([P, 3], F32, name="spread")
             nc.scalar.activation(
-                out=unread[:], in_=unit[:, i, 0, :], func=ACT.Square, bias=minus_mean[i][:, 1:2],
+                out=unread[:, D : 2 * D], in_=unit[:, i, 0, :], func=ACT.Square, bias=minus_mean[i][:, 1:2],
                 accum_out=spread[i][:, 2:3],
             )
             for h in range(HALVES):
                 nc.scalar.activation(
-                    out=unread[:, 0:BANK], in_=real_back[i][:, h, :], func=ACT.Square, bias=minus_mean[i][:, 0:1],
+                    out=unread[:, BANK * h : BANK * (h + 1)], in_=real_back[i][:, h, :], func=ACT.Square, bias=minus_mean[i][:, 0:1],
                     accum_out=spread[i][:, h : h + 1],
                 )
 
@@ -356,6 +361,7 @@ def tile_quantumcoherencelayer_kernel(
             nc.sync.dma_start(out=gain_shift_rows[0:1, 1, :], in_=ln_bias.unsqueeze(0))
 
         flipped = {}
+        ROUNDED_ON_VECTOR = (1, 2)
         EARLY_TILES = 12
         last = UNITS * TILES - 1
         with tc.tile_pool(name="stream", bufs=4) as stream, tc.tile_pool(name="work", bufs=3) as work, tc.psum_pool(
@@ -392,7 +398,8 @@ def tile_quantumcoherencelayer_kernel(
                 if n == last - 1:
                     add_magic(0, 1)
                 if n == last:
-                    take_magic_away(0)
+                    take_magic_away(0, 0)
+                    take_magic_away(0, 1)
                 if n == last + 1:
                     nc.scalar.activation(out=table_warmer[:], in_=one_col[:], func=ACT.Sin)
                     turns[0] = work.tile([P, HALVES, BANK], F32, name="linear", bufs=2)
@@ -441,10 +448,18 @@ def tile_quantumcoherencelayer_kernel(
                     layer_norm_first(i - 1)
                 if i >= 2:
                     layer_norm_second(i - 2)
+                rounds = i + 3 < TILES and i + 3 not in ROUNDED_ON_VECTOR
+                if rounds:
+                    rounded[i + 3] = angles.tile([P, HALVES, BANK], F32, name="rounded")
+                for h in range(HALVES):
+                    if here:
+                        evacuate(i, h)
+                    if rounds:
+                        add_magic(i + 3, h)
                 if here:
-                    evacuate(i)
                     unfold_real(i)
-                if i + 3 < TILES:
-                    whole_turns(i + 3)
+                if rounds:
+                    for h in range(HALVES):
+                        take_magic_away(i + 3, h)
                 if here:
                     combine_imag(i)

@@ -30,6 +30,8 @@ EPS = 1e-8
 ROUND_MAGIC = 12582912.0
 TWO_PI = 2.0 * math.pi
 
+EARLY_TILES = 12
+
 FLOPS = 2 * TOKENS * D * D
 
 
@@ -66,8 +68,11 @@ def tile_quantumcoherencelayer_kernel(
         table_warmer = keep.tile([P, 1], F32)
         minus_half = keep.tile([P, 2], F32)
         phase_sums = keep.tile([P, 2, HALVES, TILES], F32)
-        turns_per_unit = keep.tile([P, TILES], F32)
-        gain_rows = keep.tile([P, D], BF16)
+        turns_early = keep.tile([P, EARLY_TILES], F32)
+        turns_late = keep.tile([P, TILES - EARLY_TILES], F32)
+        shift_rows = keep.tile([P, D], BF16)
+        identity_bf = keep.tile([P, P], BF16)
+        weight_cols = keep.tile([P, BLOCKS * HALVES], F32)
         spare = keep.tile([P, 2, D], F32)
 
         nc.vector.memset(one_col[:], 1.0)
@@ -80,6 +85,7 @@ def tile_quantumcoherencelayer_kernel(
         nc.vector.memset(gain_shift_rows[:], 0.0)
         nc.vector.memset(w_scales[:].rearrange("p g n -> p (g n)").bitcast(I32), 0)
         make_identity(nc, identity[:])
+        nc.vector.tensor_copy(out=identity_bf[:], in_=identity[:])
         nc.scalar.activation(out=table_warmer[:], in_=one_col[:], func=ACT.Abs_reciprocal_sqrt)
 
         x_in, squared, linear, grouped, folded, inverse_t, unfolded = {}, {}, {}, {}, {}, {}, {}
@@ -162,7 +168,7 @@ def tile_quantumcoherencelayer_kernel(
             if shifted:
                 for part in range(2):
                     nc.vector.scalar_tensor_tensor(
-                        out=gain_rows[:, BANK * part : BANK * (part + 1)], in0=x_in[i][:, part, cols], scalar=EPS, in1=unfolded[n][:, 0, :],
+                        out=shift_rows[:, BANK * part : BANK * (part + 1)], in0=x_in[i][:, part, cols], scalar=EPS, in1=unfolded[n][:, 0, :],
                         op0=ALU.add, op1=ALU.mult, accum_out=phase_sums[:, part, h, i : i + 1],
                     )
             else:
@@ -182,7 +188,7 @@ def tile_quantumcoherencelayer_kernel(
                 quantise(i)
 
         sums, rounded, turns, cos_sin, real, total, minus_mean, spread, inv_std = {}, {}, {}, {}, {}, {}, {}, {}, {}
-        real_t, real_t_rows, real_back = {}, {}, {}
+        real_t, real_t_rows, real_back, squares_t, variance, result, mean_square = {}, {}, {}, {}, {}, {}, {}
 
         def multiply(i, banks):
             sums[i] = banks
@@ -203,31 +209,43 @@ def tile_quantumcoherencelayer_kernel(
             both = psum.tile([P, HALVES, BANK], F32, name="sums")
             return [both[:, h, :] for h in range(HALVES)]
 
+        def turns_per_unit(i):
+            return turns_early[:, i : i + 1] if i < EARLY_TILES else turns_late[:, i - EARLY_TILES : i - EARLY_TILES + 1]
+
+        def on_vector(i, h):
+            return i in (1, 2) or (i > 3 and h == 1)
+
         def add_magic(i, h):
             nc.scalar.activation(
-                out=rounded[i][:, h, :], in_=sums[i][h], func=ACT.Identity,
-                scale=turns_per_unit[:, i : i + 1], bias=magic_col[:],
+                out=rounded[i, h], in_=sums[i][h], func=ACT.Identity,
+                scale=turns_per_unit(i), bias=magic_col[:],
             )
 
         def take_magic_away(i, h):
-            nc.scalar.activation(
-                out=rounded[i][:, h, :], in_=rounded[i][:, h, :], func=ACT.Identity, bias=minus_magic_col[:]
-            )
+            if on_vector(i, h):
+                return
+            nc.scalar.activation(out=rounded[i, h], in_=rounded[i, h], func=ACT.Identity, bias=minus_magic_col[:])
+
+        def rounded_by_scalar(i, h):
+            if on_vector(i, h):
+                return
+            by_scalar = angles.tile([P, BANK], F32, name="by_scalar")
+            rounded[i, h] = by_scalar[:]
+            add_magic(i, h)
 
         def whole_turns_on_vector(i):
-            rounded[i] = angles.tile([P, HALVES, BANK], I32, name="rounded")
             for h in range(HALVES):
-                nc.vector.tensor_scalar_mul(
-                    out=rounded[i][:, h, :], in0=sums[i][h], scalar1=turns_per_unit[:, i : i + 1]
-                )
+                if on_vector(i, h):
+                    by_vector = angles.tile([P, BANK], I32, name="by_vector")
+                    rounded[i, h] = by_vector[:]
+                    nc.vector.tensor_scalar_mul(out=rounded[i, h], in0=sums[i][h], scalar1=turns_per_unit(i))
 
         def wrap(i):
-            if i in ROUNDED_ON_VECTOR:
-                whole_turns_on_vector(i)
+            whole_turns_on_vector(i)
             for h in range(HALVES):
                 nc.vector.scalar_tensor_tensor(
-                    out=turns[i][:, h, :], in0=sums[i][h], scalar=turns_per_unit[:, i : i + 1],
-                    in1=rounded[i][:, h, :], op0=ALU.mult, op1=ALU.subtract,
+                    out=turns[i][:, h, :], in0=sums[i][h], scalar=turns_per_unit(i),
+                    in1=rounded[i, h], op0=ALU.mult, op1=ALU.subtract,
                 )
 
         def cos_and_sin(i):
@@ -239,109 +257,147 @@ def tile_quantumcoherencelayer_kernel(
             )
 
         def straight_products(i):
-            real[i] = spare if i % 4 == 3 else results.tile([P, 2, D], F32, name="real")
+            real[i] = spare if i % 2 == 1 else results.tile([P, 2, D], F32, name="real", bufs=1)
             total[i] = small.tile([P, 3], F32, name="total")
-            minus_mean[i] = small.tile([P, 2], F32, name="minus_mean")
-            for part, sign in enumerate((1.0, -1.0)):
+            for part in (1, 0) if cross_on_vector(i, 1) else (0, 1):
                 nc.vector.scalar_tensor_tensor(
-                    out=real[i][:, part, :], in0=unit[:, i, part, :], scalar=sign, in1=cos_sin[i][:, part, :],
-                    op0=ALU.mult, op1=ALU.mult, accum_out=total[i][:, part : part + 1],
+                    out=real[i][:, part, :], in0=unit[:, i, part, :], scalar=(1.0, -1.0)[part],
+                    in1=cos_sin[i][:, part, :], op0=ALU.mult, op1=ALU.mult, accum_out=total[i][:, part : part + 1],
                 )
+                if part == 1 and cross_on_vector(i, 1):
+                    cross_product(i, 1)
 
         def fold_real(i):
             real_t[i] = psum.tile([P, HALVES, BANK], F32, name="real_t")
             for h in range(HALVES):
                 for block in range(BLOCKS):
                     cols = slice(BANK * h + P * block, BANK * h + P * (block + 1))
-                    for part in range(2):
+                    terms = (real[i][:, 0, cols], real[i][:, 1, cols], minus_mean[i][:, 0:1].to_broadcast([P, P]))
+                    for t, term in enumerate(terms):
                         nc.tensor.matmul(
-                            out=real_t[i][:, h, P * block : P * (block + 1)], lhsT=real[i][:, part, cols],
-                            rhs=identity[:], is_transpose=True, start=(part == 0), stop=(part == 1),
+                            out=real_t[i][:, h, P * block : P * (block + 1)], lhsT=term,
+                            rhs=identity[:], is_transpose=True, start=(t == 0), stop=(t == len(terms) - 1),
                         )
 
         def evacuate(i, h):
             if h == 0:
-                real_t_rows[i] = turned.tile([P, HALVES, BANK], F32, name="real_t_rows")
-            nc.scalar.copy(out=real_t_rows[i][:, h, :], in_=real_t[i][:, h, :])
+                squares_t[i] = turned.tile([P, HALVES, BANK], F32, name="squares_t", bufs=1)
+                real_t_rows[i] = turned.tile([P, HALVES, BANK], F32, name="real_t_rows", bufs=2)
+            nc.scalar.activation(out=squares_t[i][:, h, :], in_=real_t[i][:, h, :], func=ACT.Square, scale=float(D))
+            for block in range(BLOCKS):
+                cols = slice(P * block, P * (block + 1))
+                nc.scalar.activation(
+                    out=real_t_rows[i][:, h, cols], in_=real_t[i][:, h, cols], func=ACT.Copy,
+                    scale=weight_cols[:, BLOCKS * h + block : BLOCKS * h + block + 1],
+                )
 
-        def unfold_real(i):
-            real_back[i] = psum.tile([P, HALVES, BANK], F32, name="real_back")
+        def sum_squares(i):
+            variance[i] = psum.tile([P, BANK], F32, name="variance")
             for h in range(HALVES):
                 for block in range(BLOCKS):
-                    cols = slice(P * block, P * (block + 1))
-                    nc.tensor.transpose(real_back[i][:, h, cols], real_t_rows[i][:, h, cols], identity[:])
+                    nc.tensor.matmul(
+                        out=variance[i][:, 0:P], lhsT=squares_t[i][:, h, P * block : P * (block + 1)], rhs=identity[:],
+                        is_transpose=True, start=(h == 0 and block == 0), stop=(h == HALVES - 1 and block == BLOCKS - 1),
+                    )
 
-        def cross_products(i):
-            for part in range(2):
-                nc.gpsimd.tensor_tensor(
-                    out=unit[:, i, part, :], in0=unit[:, i, part, :], in1=cos_sin[i][:, 1 - part, :], op=ALU.mult
-                )
+        def unfold_real(i, h):
+            real_back[i] = psum.tile([P, BANK], F32, name="real_back")
+            for block in range(BLOCKS):
+                cols = slice(P * block, P * (block + 1))
+                nc.tensor.transpose(real_back[i][:, cols], real_t_rows[i][:, h, cols], identity[:])
+
+        def cross_on_vector(i, part):
+            return part == 1 and i in (0, 1, TILES - 1)
+
+        def cross_product(i, part):
+            engine = nc.vector if cross_on_vector(i, part) else nc.gpsimd
+            engine.tensor_tensor(
+                out=unit[:, i, part, :], in0=unit[:, i, part, :], in1=cos_sin[i][:, 1 - part, :], op=ALU.mult
+            )
 
         def combine_imag(i):
             nc.vector.scalar_tensor_tensor(
                 out=unit[:, i, 0, :], in0=unit[:, i, 0, :], scalar=1.0, in1=unit[:, i, 1, :],
                 op0=ALU.mult, op1=ALU.add, accum_out=total[i][:, 2:3],
             )
-            nc.vector.tensor_scalar(
-                out=minus_mean[i][:, 0:1], in0=total[i][:, 0:1], scalar1=total[i][:, 1:2], scalar2=-1.0 / D,
-                op0=ALU.add, op1=ALU.mult,
-            )
-            nc.vector.tensor_scalar_mul(out=minus_mean[i][:, 1:2], in0=total[i][:, 2:3], scalar1=-1.0 / D)
 
-        def spreads(i):
-            unread = small.tile([P, 2 * D], BF16, name="unread", bufs=1)
-            spread[i] = small.tile([P, 3], F32, name="spread")
+        def real_mean_first(i):
+            minus_mean[i] = small.tile([P, 3], F32, name="minus_mean")
             nc.scalar.activation(
-                out=unread[:, D : 2 * D], in_=unit[:, i, 0, :], func=ACT.Square, bias=minus_mean[i][:, 1:2],
-                accum_out=spread[i][:, 2:3],
+                out=minus_mean[i][:, 2:3], in_=total[i][:, 0:1], func=ACT.Copy, scale=-1.0 / D
             )
-            for h in range(HALVES):
-                nc.scalar.activation(
-                    out=unread[:, BANK * h : BANK * (h + 1)], in_=real_back[i][:, h, :], func=ACT.Square, bias=minus_mean[i][:, 0:1],
-                    accum_out=spread[i][:, h : h + 1],
-                )
+
+        def real_mean_second(i):
+            nc.scalar.activation(
+                out=minus_mean[i][:, 0:1], in_=total[i][:, 1:2], func=ACT.Identity, scale=-1.0 / D,
+                bias=minus_mean[i][:, 2:3],
+            )
+
+        def imag_mean(i):
+            nc.scalar.activation(out=minus_mean[i][:, 1:2], in_=total[i][:, 2:3], func=ACT.Copy, scale=-1.0 / D)
+
+        def imag_spread(i):
+            unread = small.tile([P, D], BF16, name="unread", bufs=1)
+            spread[i] = small.tile([P, 2], F32, name="spread")
+            nc.scalar.activation(
+                out=unread[:], in_=unit[:, i, 0, :], func=ACT.Square, scale=-float(D), bias=total[i][:, 2:3],
+                accum_out=spread[i][:, 1:2],
+            )
+
+        def real_spread(i):
+            unread = small.tile([P, P], BF16, name="unread_sum", bufs=1)
+            nc.scalar.activation(
+                out=unread[:], in_=variance[i][:, 0:P], func=ACT.Identity, accum_out=spread[i][:, 0:1]
+            )
+
+        def mean_squares(i):
+            mean_square[i] = small.tile([P, 2], F32, name="mean_square")
+            nc.scalar.activation(
+                out=mean_square[i][:], in_=spread[i][:], func=ACT.Identity, scale=1.0 / D**3, bias=eps_col[:]
+            )
 
         def deviations(i):
             inv_std[i] = small.tile([P, 2], F32, name="inv_std")
-            nc.gpsimd.tensor_tensor(out=spread[i][:, 1:2], in0=spread[i][:, 0:1], in1=spread[i][:, 1:2], op=ALU.add)
-            nc.gpsimd.tensor_scalar(
-                out=spread[i][:, 1:3], in0=spread[i][:, 1:3], scalar1=1.0 / D, scalar2=EPS, op0=ALU.mult, op1=ALU.add
-            )
-            nc.gpsimd.tensor_tensor(out=inv_std[i][:], in0=spread[i][:, 1:3], in1=minus_half[:], op=ALU.pow)
+            nc.gpsimd.tensor_tensor(out=inv_std[i][:], in0=mean_square[i][:], in1=minus_half[:], op=ALU.pow)
 
-        def layer_norm_first(i):
-            for h in range(HALVES):
-                cols = slice(BANK * h, BANK * (h + 1))
-                nc.vector.scalar_tensor_tensor(
-                    out=real[i][:, 0, cols], in0=real_back[i][:, h, :], scalar=minus_mean[i][:, 0:1],
-                    in1=gain_rows[:, cols], op0=ALU.add, op1=ALU.mult,
-                )
+        def layer_norm_real(i, h):
+            if h == 0:
+                result[i] = results.tile([P, D], F32, name="result", bufs=2)
+            cols = slice(BANK * h, BANK * (h + 1))
+            nc.vector.scalar_tensor_tensor(
+                out=result[i][:, cols], in0=real_back[i][:], scalar=inv_std[i][:, 0:1], in1=shift_rows[:, cols],
+                op0=ALU.mult, op1=ALU.add,
+            )
+            if i == TILES - 1:
+                nc.sync.dma_start(out=out_dram[0][:, i, cols], in_=result[i][:, cols])
+            elif h == HALVES - 1:
+                nc.sync.dma_start(out=out_dram[0][:, i, :], in_=result[i][:])
+
+        def layer_norm_imag_first(i):
             nc.vector.scalar_tensor_tensor(
                 out=unit[:, i, 0, :], in0=unit[:, i, 0, :], scalar=minus_mean[i][:, 1:2], in1=gain[:],
                 op0=ALU.add, op1=ALU.mult,
             )
 
-        def layer_norm_second(i):
-            for part, values in enumerate((real[i][:, 0, :], unit[:, i, 0, :])):
-                nc.vector.scalar_tensor_tensor(
-                    out=values, in0=values, scalar=inv_std[i][:, part : part + 1], in1=shift[:],
-                    op0=ALU.mult, op1=ALU.add,
-                )
-                nc.sync.dma_start(out=out_dram[part][:, i, :], in_=values)
+        def layer_norm_imag_second(i):
+            values = unit[:, i, 0, :]
+            nc.vector.scalar_tensor_tensor(
+                out=values, in0=values, scalar=inv_std[i][:, 1:2], in1=shift[:], op0=ALU.mult, op1=ALU.add
+            )
+            nc.sync.dma_start(out=out_dram[1][:, i, :], in_=values)
 
-        def turns_of(tiles):
+        def turns_of(engine, tiles, turns_column):
             whole_sums = phase_sums[:, :, 0, tiles]
-            nc.vector.tensor_tensor(out=whole_sums, in0=whole_sums, in1=phase_sums[:, :, 1, tiles], op=ALU.add)
-            nc.vector.tensor_tensor(out=whole_sums, in0=whole_sums, in1=whole_sums, op=ALU.mult)
-            nc.vector.tensor_tensor(
-                out=turns_per_unit[:, tiles], in0=phase_sums[:, 0, 0, tiles], in1=phase_sums[:, 1, 0, tiles], op=ALU.add
+            engine.tensor_tensor(out=whole_sums, in0=whole_sums, in1=phase_sums[:, :, 1, tiles], op=ALU.add)
+            engine.tensor_tensor(out=whole_sums, in0=whole_sums, in1=whole_sums, op=ALU.mult)
+            engine.tensor_tensor(
+                out=turns_column[:], in0=phase_sums[:, 0, 0, tiles], in1=phase_sums[:, 1, 0, tiles], op=ALU.add
             )
-            nc.vector.tensor_scalar(
-                out=turns_per_unit[:, tiles], in0=turns_per_unit[:, tiles], scalar1=-1.0 / (D * D), scalar2=1.0,
-                op0=ALU.mult, op1=ALU.add,
+            engine.tensor_scalar(
+                out=turns_column[:], in0=turns_column[:], scalar1=-1.0 / (D * D), scalar2=1.0, op0=ALU.mult, op1=ALU.add
             )
-            nc.vector.tensor_scalar(
-                out=turns_per_unit[:, tiles], in0=turns_per_unit[:, tiles], scalar1=factor[:], scalar2=1.0 / TWO_PI,
+            engine.tensor_scalar(
+                out=turns_column[:], in0=turns_column[:], scalar1=factor[:], scalar2=1.0 / TWO_PI,
                 op0=ALU.mult, op1=ALU.mult,
             )
 
@@ -360,9 +416,15 @@ def tile_quantumcoherencelayer_kernel(
             nc.sync.dma_start(out=gain_shift_rows[0:1, 0, :], in_=ln_weight.unsqueeze(0))
             nc.sync.dma_start(out=gain_shift_rows[0:1, 1, :], in_=ln_bias.unsqueeze(0))
 
+        def turn_weight():
+            weight_t = psum1.tile([P, BLOCKS * HALVES, P], BF16, name="flipped", bufs=2)
+            for block in range(BLOCKS * HALVES):
+                nc.tensor.transpose(
+                    weight_t[:, block, :], gain_shift_rows[:, 0, P * block : P * (block + 1)], identity_bf[:]
+                )
+            nc.vector.tensor_copy(out=weight_cols[:], in_=weight_t[:, :, 0])
+
         flipped = {}
-        ROUNDED_ON_VECTOR = (1, 2)
-        EARLY_TILES = 12
         last = UNITS * TILES - 1
         with tc.tile_pool(name="stream", bufs=4) as stream, tc.tile_pool(name="work", bufs=3) as work, tc.psum_pool(
             name="psum1", bufs=3
@@ -389,11 +451,14 @@ def tile_quantumcoherencelayer_kernel(
                     load_the_rest()
                 if n == UNITS * (EARLY_TILES + 1) + 2:
                     nc.vector.tensor_copy(out=factor[:], in_=factor_bf[:])
-                    turns_of(slice(0, EARLY_TILES))
+                    turns_of(nc.vector, slice(0, EARLY_TILES), turns_early)
+                if n == UNITS * EARLY_TILES + 2:
+                    turn_weight()
                 if n == last - 3:
                     multiply(0, [psum1.tile([P, BANK], F32, name="flipped", bufs=2)[:] for h in range(HALVES)])
                 if n == last - 2:
-                    rounded[0] = work.tile([P, HALVES, BANK], F32, name="linear", bufs=2)
+                    early = work.tile([P, HALVES, BANK], F32, name="linear", bufs=2)
+                    rounded[0, 0], rounded[0, 1] = early[:, 0, :], early[:, 1, :]
                     add_magic(0, 0)
                 if n == last - 1:
                     add_magic(0, 1)
@@ -410,7 +475,7 @@ def tile_quantumcoherencelayer_kernel(
 
         with tc.psum_pool(name="psum", bufs=1) as psum, tc.tile_pool(
             name="angles", bufs=2, reuse_waits="tile"
-        ) as angles, tc.tile_pool(name="results", bufs=3, reuse_waits="tile") as results, tc.tile_pool(
+        ) as angles, tc.tile_pool(name="results", bufs=2, reuse_waits="tile") as results, tc.tile_pool(
             name="small", bufs=4, reuse_waits="tile"
         ) as small, tc.tile_pool(name="turned", bufs=1) as turned:
             multiply(1, sums_banks())
@@ -422,44 +487,60 @@ def tile_quantumcoherencelayer_kernel(
                     nc.tensor.matmul(
                         out=repeated[:, n_cols], lhsT=ones[:], rhs=gain_shift_rows[:, row, n_cols], start=True, stop=True
                     )
-            turns_of(slice(EARLY_TILES, TILES))
-            nc.vector.tensor_copy(out=gain_rows[:], in_=gain[:])
+            nc.scalar.copy(out=shift_rows[:], in_=shift[:])
+            turns_of(nc.gpsimd, slice(EARLY_TILES, TILES), turns_late)
 
             for i in range(-2, TILES + 2):
-                here = 0 <= i < TILES
+                here, before, two_before = 0 <= i < TILES, 1 <= i <= TILES, i >= 2
+                ahead = i + 3 < TILES
+                if i == TILES - 1:
+                    deviations(i - 2)
                 if here:
                     straight_products(i)
-                    fold_real(i)
+                    cross_product(i, 0)
+                if before:
+                    imag_mean(i - 1)
+                    fold_real(i - 1)
+                    imag_spread(i - 1)
+                    evacuate(i - 1, 0)
+                    evacuate(i - 1, 1)
                 if 1 <= i + 2 < TILES:
                     turns[i + 2] = angles.tile([P, HALVES, BANK], F32, name="turns")
                     wrap(i + 2)
+                if before:
+                    layer_norm_imag_first(i - 1)
+                if two_before:
+                    if i != TILES - 1:
+                        deviations(i - 2)
+                    layer_norm_real(i - 2, 0)
+                    unfold_real(i - 2, 1)
+                if here and not cross_on_vector(i, 1):
+                    cross_product(i, 1)
                 if 2 <= i + 3 < TILES:
                     multiply(i + 3, sums_banks())
-                if 1 <= i <= TILES:
-                    spreads(i - 1)
-                if here:
-                    cross_products(i)
-                if 1 <= i <= TILES:
-                    deviations(i - 1)
+                if before:
+                    sum_squares(i - 1)
                 if 1 <= i + 1 < TILES:
                     cos_sin[i + 1] = angles.tile([P, 2, D], F32, name="cos_sin")
                     cos_and_sin(i + 1)
-                if 1 <= i <= TILES:
-                    layer_norm_first(i - 1)
-                if i >= 2:
-                    layer_norm_second(i - 2)
-                rounds = i + 3 < TILES and i + 3 not in ROUNDED_ON_VECTOR
-                if rounds:
-                    rounded[i + 3] = angles.tile([P, HALVES, BANK], F32, name="rounded")
-                for h in range(HALVES):
-                    if here:
-                        evacuate(i, h)
-                    if rounds:
-                        add_magic(i + 3, h)
                 if here:
-                    unfold_real(i)
-                if rounds:
-                    for h in range(HALVES):
-                        take_magic_away(i + 3, h)
+                    real_mean_first(i)
+                if ahead:
+                    rounded_by_scalar(i + 3, 0)
+                    rounded_by_scalar(i + 3, 1)
+                if here:
+                    real_mean_second(i)
+                if before:
+                    real_spread(i - 1)
+                if ahead:
+                    take_magic_away(i + 3, 0)
+                    take_magic_away(i + 3, 1)
+                if before:
+                    mean_squares(i - 1)
+                if two_before:
+                    layer_norm_imag_second(i - 2)
+                    layer_norm_real(i - 2, 1)
+                if before:
+                    unfold_real(i - 1, 0)
                 if here:
                     combine_imag(i)

@@ -188,7 +188,7 @@ def tile_quantumcoherencelayer_kernel(
                 quantise(i)
 
         sums, rounded, turns, cos_sin, real, total, minus_mean, spread, inv_std = {}, {}, {}, {}, {}, {}, {}, {}, {}
-        real_t, real_t_rows, real_back, squares_t, variance, result, mean_square = {}, {}, {}, {}, {}, {}, {}
+        real_t, real_t_rows, real_back, squares_t, variance, result, mean_square, minus_real_mean = {}, {}, {}, {}, {}, {}, {}, {}
 
         def multiply(i, banks):
             sums[i] = banks
@@ -213,7 +213,7 @@ def tile_quantumcoherencelayer_kernel(
             return turns_early[:, i : i + 1] if i < EARLY_TILES else turns_late[:, i - EARLY_TILES : i - EARLY_TILES + 1]
 
         def on_vector(i, h):
-            return i in (1, 2) or (i > 3 and h == 1)
+            return i in (1, 2) or (i > 3 and (h == 1 or i % 2 == 0))
 
         def add_magic(i, h):
             nc.scalar.activation(
@@ -272,7 +272,7 @@ def tile_quantumcoherencelayer_kernel(
             for h in range(HALVES):
                 for block in range(BLOCKS):
                     cols = slice(BANK * h + P * block, BANK * h + P * (block + 1))
-                    terms = (real[i][:, 0, cols], real[i][:, 1, cols], minus_mean[i][:, 0:1].to_broadcast([P, P]))
+                    terms = (real[i][:, 0, cols], real[i][:, 1, cols], minus_real_mean[i][:].to_broadcast([P, P]))
                     for t, term in enumerate(terms):
                         nc.tensor.matmul(
                             out=real_t[i][:, h, P * block : P * (block + 1)], lhsT=term,
@@ -321,20 +321,16 @@ def tile_quantumcoherencelayer_kernel(
                 op0=ALU.mult, op1=ALU.add, accum_out=total[i][:, 2:3],
             )
 
-        def real_mean_first(i):
-            minus_mean[i] = small.tile([P, 3], F32, name="minus_mean")
-            nc.scalar.activation(
-                out=minus_mean[i][:, 2:3], in_=total[i][:, 0:1], func=ACT.Copy, scale=-1.0 / D
-            )
-
-        def real_mean_second(i):
-            nc.scalar.activation(
-                out=minus_mean[i][:, 0:1], in_=total[i][:, 1:2], func=ACT.Identity, scale=-1.0 / D,
-                bias=minus_mean[i][:, 2:3],
+        def real_mean(i):
+            minus_real_mean[i] = small.tile([P, 1], F32, name="minus_real_mean")
+            nc.gpsimd.tensor_scalar(
+                out=minus_real_mean[i][:], in0=total[i][:, 0:1], scalar1=total[i][:, 1:2], scalar2=-1.0 / D,
+                op0=ALU.add, op1=ALU.mult,
             )
 
         def imag_mean(i):
-            nc.scalar.activation(out=minus_mean[i][:, 1:2], in_=total[i][:, 2:3], func=ACT.Copy, scale=-1.0 / D)
+            minus_mean[i] = small.tile([P, 1], F32, name="minus_mean")
+            nc.scalar.activation(out=minus_mean[i][:], in_=total[i][:, 2:3], func=ACT.Copy, scale=-1.0 / D)
 
         def imag_spread(i):
             unread = small.tile([P, D], BF16, name="unread", bufs=1)
@@ -375,7 +371,7 @@ def tile_quantumcoherencelayer_kernel(
 
         def layer_norm_imag_first(i):
             nc.vector.scalar_tensor_tensor(
-                out=unit[:, i, 0, :], in0=unit[:, i, 0, :], scalar=minus_mean[i][:, 1:2], in1=gain[:],
+                out=unit[:, i, 0, :], in0=unit[:, i, 0, :], scalar=minus_mean[i][:], in1=gain[:],
                 op0=ALU.add, op1=ALU.mult,
             )
 
@@ -514,8 +510,10 @@ def tile_quantumcoherencelayer_kernel(
                         deviations(i - 2)
                     layer_norm_real(i - 2, 0)
                     unfold_real(i - 2, 1)
-                if here and not cross_on_vector(i, 1):
-                    cross_product(i, 1)
+                if here:
+                    real_mean(i)
+                    if not cross_on_vector(i, 1):
+                        cross_product(i, 1)
                 if 2 <= i + 3 < TILES:
                     multiply(i + 3, sums_banks())
                 if before:
@@ -523,13 +521,9 @@ def tile_quantumcoherencelayer_kernel(
                 if 1 <= i + 1 < TILES:
                     cos_sin[i + 1] = angles.tile([P, 2, D], F32, name="cos_sin")
                     cos_and_sin(i + 1)
-                if here:
-                    real_mean_first(i)
                 if ahead:
                     rounded_by_scalar(i + 3, 0)
                     rounded_by_scalar(i + 3, 1)
-                if here:
-                    real_mean_second(i)
                 if before:
                     real_spread(i - 1)
                 if ahead:

@@ -118,9 +118,12 @@ def tile_quantumcoherencelayer_kernel(
 
         def linear_terms(i):
             linear[i] = work.tile([P, 2, D], F32, name="linear", bufs=2)
-            nc.gpsimd.tensor_scalar(
-                out=linear[i][:], in0=x_in[i][:], scalar1=2.0 * EPS, scalar2=EPS * EPS, op0=ALU.mult, op1=ALU.add
-            )
+            pieces = (slice(0, BANK), slice(BANK, D)) if i == 0 else (slice(0, D),)
+            for cols in pieces:
+                nc.gpsimd.tensor_scalar(
+                    out=linear[i][:, :, cols], in0=x_in[i][:, :, cols], scalar1=2.0 * EPS, scalar2=EPS * EPS,
+                    op0=ALU.mult, op1=ALU.add,
+                )
 
         def quantise(i):
             nc.vector.quantize_mx(
@@ -213,7 +216,7 @@ def tile_quantumcoherencelayer_kernel(
             return turns_early[:, i : i + 1] if i < EARLY_TILES else turns_late[:, i - EARLY_TILES : i - EARLY_TILES + 1]
 
         def on_vector(i, h):
-            return i in (1, 2) or (i > 3 and (h == 1 or i % 2 == 0))
+            return i > 0 and (h == 1 or i % 2 == 1 or i == 2)
 
         def add_magic(i, h):
             nc.scalar.activation(
@@ -279,11 +282,14 @@ def tile_quantumcoherencelayer_kernel(
                             rhs=identity[:], is_transpose=True, start=(t == 0), stop=(t == len(terms) - 1),
                         )
 
-        def evacuate(i, h):
+        def square_real(i, h):
             if h == 0:
                 squares_t[i] = turned.tile([P, HALVES, BANK], F32, name="squares_t", bufs=1)
-                real_t_rows[i] = turned.tile([P, HALVES, BANK], F32, name="real_t_rows", bufs=2)
             nc.scalar.activation(out=squares_t[i][:, h, :], in_=real_t[i][:, h, :], func=ACT.Square, scale=float(D))
+
+        def weigh_real(i, h):
+            if h == 0:
+                real_t_rows[i] = turned.tile([P, HALVES, BANK], F32, name="real_t_rows", bufs=2)
             for block in range(BLOCKS):
                 cols = slice(P * block, P * (block + 1))
                 nc.scalar.activation(
@@ -307,7 +313,7 @@ def tile_quantumcoherencelayer_kernel(
                 nc.tensor.transpose(real_back[i][:, cols], real_t_rows[i][:, h, cols], identity[:])
 
         def cross_on_vector(i, part):
-            return part == 1 and i in (0, 1, TILES - 1)
+            return part == 1 and i in (0, 1, TILES - 2, TILES - 1)
 
         def cross_product(i, part):
             engine = nc.vector if cross_on_vector(i, part) else nc.gpsimd
@@ -427,16 +433,22 @@ def tile_quantumcoherencelayer_kernel(
         ) as psum1:
             for i in range(3):
                 load(i)
-            for step in range(UNITS):
-                prepare(0, step)
+            for piece in range(UNITS):
+                square(0, piece)
+            linear_terms(0)
+            flip(0)
             for n in range(UNITS * TILES + 3):
                 i, step = n // UNITS, n % UNITS
                 if n < UNITS * TILES:
                     fold(n)
                 if 1 <= n <= UNITS * TILES:
                     roots(n - 1)
+                if n == 1:
+                    group(0)
                 if i + 1 < TILES:
                     prepare(i + 1, step)
+                if n == 2:
+                    quantise(0)
                 if 2 <= n <= UNITS * TILES + 1:
                     unfold(n - 2)
                 if n >= 3:
@@ -486,51 +498,48 @@ def tile_quantumcoherencelayer_kernel(
             nc.scalar.copy(out=shift_rows[:], in_=shift[:])
             turns_of(nc.gpsimd, slice(EARLY_TILES, TILES), turns_late)
 
-            for i in range(-2, TILES + 2):
-                here, before, two_before = 0 <= i < TILES, 1 <= i <= TILES, i >= 2
-                ahead = i + 3 < TILES
-                if i == TILES - 1:
-                    deviations(i - 2)
+            for i in range(-2, TILES):
+                here, before, two_before, ahead = i >= 0, i >= 1, i >= 2, i + 3 < TILES
+                ending = i >= TILES - 2
                 if here:
                     straight_products(i)
+                    if ending:
+                        real_mean(i)
                     cross_product(i, 0)
+                    if not cross_on_vector(i, 1):
+                        cross_product(i, 1)
+                    if not ending:
+                        real_mean(i)
                 if before:
                     imag_mean(i - 1)
                     fold_real(i - 1)
                     imag_spread(i - 1)
-                    evacuate(i - 1, 0)
-                    evacuate(i - 1, 1)
+                    square_real(i - 1, 0)
+                    square_real(i - 1, 1)
+                    sum_squares(i - 1)
+                    weigh_real(i - 1, 0)
+                    weigh_real(i - 1, 1)
                 if 1 <= i + 2 < TILES:
                     turns[i + 2] = angles.tile([P, HALVES, BANK], F32, name="turns")
                     wrap(i + 2)
                 if before:
                     layer_norm_imag_first(i - 1)
                 if two_before:
-                    if i != TILES - 1:
-                        deviations(i - 2)
                     layer_norm_real(i - 2, 0)
                     unfold_real(i - 2, 1)
-                if here:
-                    real_mean(i)
-                    if not cross_on_vector(i, 1):
-                        cross_product(i, 1)
                 if 2 <= i + 3 < TILES:
                     multiply(i + 3, sums_banks())
-                if before:
-                    sum_squares(i - 1)
-                if 1 <= i + 1 < TILES:
-                    cos_sin[i + 1] = angles.tile([P, 2, D], F32, name="cos_sin")
-                    cos_and_sin(i + 1)
-                if ahead:
-                    rounded_by_scalar(i + 3, 0)
-                    rounded_by_scalar(i + 3, 1)
+                trig = [t for t in {0: (1, 2), 1: ()}.get(i, (i + 1,)) if 1 <= t < TILES]
                 if before:
                     real_spread(i - 1)
-                if ahead:
-                    take_magic_away(i + 3, 0)
-                    take_magic_away(i + 3, 1)
-                if before:
                     mean_squares(i - 1)
+                    deviations(i - 1)
+                for t in trig:
+                    cos_sin[t] = angles.tile([P, 2, D], F32, name="cos_sin")
+                    cos_and_sin(t)
+                if ahead:
+                    rounded_by_scalar(i + 3, 0)
+                    take_magic_away(i + 3, 0)
                 if two_before:
                     layer_norm_imag_second(i - 2)
                     layer_norm_real(i - 2, 1)
@@ -538,3 +547,26 @@ def tile_quantumcoherencelayer_kernel(
                     unfold_real(i - 1, 0)
                 if here:
                     combine_imag(i)
+
+            last = TILES - 1
+            fold_real(last)
+            square_real(last, 0)
+            square_real(last, 1)
+            sum_squares(last)
+            imag_mean(last)
+            imag_spread(last)
+            real_spread(last)
+            layer_norm_real(last - 1, 0)
+            unfold_real(last - 1, 1)
+            mean_squares(last)
+            deviations(last)
+            layer_norm_imag_second(last - 1)
+            layer_norm_real(last - 1, 1)
+            layer_norm_imag_first(last)
+            weigh_real(last, 0)
+            weigh_real(last, 1)
+            unfold_real(last, 0)
+            layer_norm_imag_second(last)
+            layer_norm_real(last, 0)
+            unfold_real(last, 1)
+            layer_norm_real(last, 1)

@@ -251,10 +251,15 @@ def tile_quantumcoherencelayer_kernel(
                     in1=rounded[i, h], op0=ALU.mult, op1=ALU.subtract,
                 )
 
-        def cos_and_sin(i):
-            flat = "p h w -> p (h w)"
-            nc.scalar.activation(out=cos_sin[i][:, 0, :], in_=turns[i][:].rearrange(flat), func=ACT.Abs)
-            nc.scalar.activation(out=cos_sin[i][:, 1, :], in_=turns[i][:].rearrange(flat), func=ACT.Sin, scale=TWO_PI)
+        def abs_turns(i):
+            nc.scalar.activation(out=cos_sin[i][:, 0, :], in_=turns[i][:].rearrange("p h w -> p (h w)"), func=ACT.Abs)
+
+        def sine(i):
+            nc.scalar.activation(
+                out=cos_sin[i][:, 1, :], in_=turns[i][:].rearrange("p h w -> p (h w)"), func=ACT.Sin, scale=TWO_PI
+            )
+
+        def cosine(i):
             nc.scalar.activation(
                 out=cos_sin[i][:, 0, :], in_=cos_sin[i][:, 0, :], func=ACT.Sin, scale=-TWO_PI, bias=quarter_turn_col[:]
             )
@@ -479,7 +484,9 @@ def tile_quantumcoherencelayer_kernel(
                     wrap(0)
                 if n == last + 2:
                     cos_sin[0] = spare
-                    cos_and_sin(0)
+                    abs_turns(0)
+                    sine(0)
+                    cosine(0)
 
         with tc.psum_pool(name="psum", bufs=1) as psum, tc.tile_pool(
             name="angles", bufs=2, reuse_waits="tile"
@@ -501,6 +508,7 @@ def tile_quantumcoherencelayer_kernel(
             for i in range(-2, TILES):
                 here, before, two_before, ahead = i >= 0, i >= 1, i >= 2, i + 3 < TILES
                 ending = i >= TILES - 2
+                trig = [t for t in {0: (1, 2), 1: ()}.get(i, (i + 1,)) if 1 <= t < TILES]
                 if here:
                     straight_products(i)
                     if ending:
@@ -514,11 +522,12 @@ def tile_quantumcoherencelayer_kernel(
                     imag_mean(i - 1)
                     fold_real(i - 1)
                     imag_spread(i - 1)
-                    square_real(i - 1, 0)
-                    square_real(i - 1, 1)
-                    sum_squares(i - 1)
-                    weigh_real(i - 1, 0)
-                    weigh_real(i - 1, 1)
+                    for t in trig:
+                        cos_sin[t] = angles.tile([P, 2, D], F32, name="cos_sin")
+                        abs_turns(t)
+                    for h in range(HALVES):
+                        square_real(i - 1, h)
+                        weigh_real(i - 1, h)
                 if 1 <= i + 2 < TILES:
                     turns[i + 2] = angles.tile([P, HALVES, BANK], F32, name="turns")
                     wrap(i + 2)
@@ -526,20 +535,27 @@ def tile_quantumcoherencelayer_kernel(
                     layer_norm_imag_first(i - 1)
                 if two_before:
                     layer_norm_real(i - 2, 0)
-                    unfold_real(i - 2, 1)
                 if 2 <= i + 3 < TILES:
                     multiply(i + 3, sums_banks())
-                trig = [t for t in {0: (1, 2), 1: ()}.get(i, (i + 1,)) if 1 <= t < TILES]
+                if two_before:
+                    unfold_real(i - 2, 1)
                 if before:
-                    real_spread(i - 1)
-                    mean_squares(i - 1)
-                    deviations(i - 1)
+                    sum_squares(i - 1)
                 for t in trig:
-                    cos_sin[t] = angles.tile([P, 2, D], F32, name="cos_sin")
-                    cos_and_sin(t)
+                    if not before:
+                        cos_sin[t] = angles.tile([P, 2, D], F32, name="cos_sin")
+                        abs_turns(t)
+                    sine(t)
+                    cosine(t)
                 if ahead:
                     rounded_by_scalar(i + 3, 0)
+                if before:
+                    real_spread(i - 1)
+                if ahead:
                     take_magic_away(i + 3, 0)
+                if before:
+                    mean_squares(i - 1)
+                    deviations(i - 1)
                 if two_before:
                     layer_norm_imag_second(i - 2)
                     layer_norm_real(i - 2, 1)

@@ -187,10 +187,10 @@ def tile_quantumcoherencelayer_kernel(
                 flip(i)
             if step == 1:
                 group(i)
-            if step == 2:
+            if step == 3:
                 quantise(i)
 
-        sums, rounded, turns, cos_sin, real, total, minus_mean, spread, inv_std = {}, {}, {}, {}, {}, {}, {}, {}, {}
+        sums, rounded, turns, sin_cos, real, total, minus_mean, spread, inv_std = {}, {}, {}, {}, {}, {}, {}, {}, {}
         real_t, real_t_rows, real_back, squares_t, variance, result, mean_square, minus_real_mean = {}, {}, {}, {}, {}, {}, {}, {}
 
         def multiply(i, banks):
@@ -252,40 +252,40 @@ def tile_quantumcoherencelayer_kernel(
                 )
 
         def abs_turns(i):
-            nc.scalar.activation(out=cos_sin[i][:, 0, :], in_=turns[i][:].rearrange("p h w -> p (h w)"), func=ACT.Abs)
+            nc.scalar.activation(out=sin_cos[i][:, 1, :], in_=turns[i][:].rearrange("p h w -> p (h w)"), func=ACT.Abs)
 
         def sine(i):
             nc.scalar.activation(
-                out=cos_sin[i][:, 1, :], in_=turns[i][:].rearrange("p h w -> p (h w)"), func=ACT.Sin, scale=TWO_PI
+                out=sin_cos[i][:, 0, :], in_=turns[i][:].rearrange("p h w -> p (h w)"), func=ACT.Sin, scale=TWO_PI
             )
 
         def cosine(i):
             nc.scalar.activation(
-                out=cos_sin[i][:, 0, :], in_=cos_sin[i][:, 0, :], func=ACT.Sin, scale=-TWO_PI, bias=quarter_turn_col[:]
+                out=sin_cos[i][:, 1, :], in_=sin_cos[i][:, 1, :], func=ACT.Sin, scale=-TWO_PI, bias=quarter_turn_col[:]
             )
 
         def straight_products(i):
             real[i] = spare if i % 2 == 1 else results.tile([P, 2, D], F32, name="real", bufs=1)
             total[i] = small.tile([P, 3], F32, name="total")
-            for part in (1, 0) if cross_on_vector(i, 1) else (0, 1):
+            for part in (1, 0) if b_cos_on_vector(i) else (0, 1):
                 nc.vector.scalar_tensor_tensor(
                     out=real[i][:, part, :], in0=unit[:, i, part, :], scalar=(1.0, -1.0)[part],
-                    in1=cos_sin[i][:, part, :], op0=ALU.mult, op1=ALU.mult, accum_out=total[i][:, part : part + 1],
+                    in1=sin_cos[i][:, 1 - part, :], op0=ALU.mult, op1=ALU.mult, accum_out=total[i][:, part : part + 1],
                 )
-                if part == 1 and cross_on_vector(i, 1):
-                    cross_product(i, 1)
+                if part == 1 and b_cos_on_vector(i):
+                    b_cos(i)
 
-        def fold_real(i):
-            real_t[i] = psum.tile([P, HALVES, BANK], F32, name="real_t")
-            for h in range(HALVES):
-                for block in range(BLOCKS):
-                    cols = slice(BANK * h + P * block, BANK * h + P * (block + 1))
-                    terms = (real[i][:, 0, cols], real[i][:, 1, cols], minus_real_mean[i][:].to_broadcast([P, P]))
-                    for t, term in enumerate(terms):
-                        nc.tensor.matmul(
-                            out=real_t[i][:, h, P * block : P * (block + 1)], lhsT=term,
-                            rhs=identity[:], is_transpose=True, start=(t == 0), stop=(t == len(terms) - 1),
-                        )
+        def fold_real(i, h):
+            if h == 0:
+                real_t[i] = psum.tile([P, HALVES, BANK], F32, name="real_t")
+            for block in range(BLOCKS):
+                cols = slice(BANK * h + P * block, BANK * h + P * (block + 1))
+                terms = (real[i][:, 0, cols], real[i][:, 1, cols], minus_real_mean[i][:].to_broadcast([P, P]))
+                for t, term in enumerate(terms):
+                    nc.tensor.matmul(
+                        out=real_t[i][:, h, P * block : P * (block + 1)], lhsT=term,
+                        rhs=identity[:], is_transpose=True, start=(t == 0), stop=(t == len(terms) - 1),
+                    )
 
         def square_real(i, h):
             if h == 0:
@@ -312,18 +312,24 @@ def tile_quantumcoherencelayer_kernel(
                     )
 
         def unfold_real(i, h):
-            real_back[i] = psum.tile([P, BANK], F32, name="real_back")
+            if i == TILES - 1 and h == 1:
+                real_back[i, h] = psum.tile([P, BANK], F32, name="variance")
+            else:
+                real_back[i, h] = psum.tile([P, BANK], F32, name="real_back")
             for block in range(BLOCKS):
                 cols = slice(P * block, P * (block + 1))
-                nc.tensor.transpose(real_back[i][:, cols], real_t_rows[i][:, h, cols], identity[:])
+                nc.tensor.transpose(real_back[i, h][:, cols], real_t_rows[i][:, h, cols], identity[:])
 
-        def cross_on_vector(i, part):
-            return part == 1 and i in (0, 1, TILES - 2, TILES - 1)
+        def b_cos_on_vector(i):
+            return i in (0, 1, TILES - 2, TILES - 1)
 
-        def cross_product(i, part):
-            engine = nc.vector if cross_on_vector(i, part) else nc.gpsimd
-            engine.tensor_tensor(
-                out=unit[:, i, part, :], in0=unit[:, i, part, :], in1=cos_sin[i][:, 1 - part, :], op=ALU.mult
+        def b_cos(i):
+            nc.vector.tensor_tensor(out=unit[:, i, 1, :], in0=unit[:, i, 1, :], in1=sin_cos[i][:, 1, :], op=ALU.mult)
+
+        def cross_products(i):
+            parts = slice(0, 1) if b_cos_on_vector(i) else slice(0, 2)
+            nc.gpsimd.tensor_tensor(
+                out=unit[:, i, parts, :], in0=unit[:, i, parts, :], in1=sin_cos[i][:, parts, :], op=ALU.mult
             )
 
         def combine_imag(i):
@@ -372,7 +378,7 @@ def tile_quantumcoherencelayer_kernel(
                 result[i] = results.tile([P, D], F32, name="result", bufs=2)
             cols = slice(BANK * h, BANK * (h + 1))
             nc.vector.scalar_tensor_tensor(
-                out=result[i][:, cols], in0=real_back[i][:], scalar=inv_std[i][:, 0:1], in1=shift_rows[:, cols],
+                out=result[i][:, cols], in0=real_back[i, h][:], scalar=inv_std[i][:, 0:1], in1=shift_rows[:, cols],
                 op0=ALU.mult, op1=ALU.add,
             )
             if i == TILES - 1:
@@ -483,7 +489,7 @@ def tile_quantumcoherencelayer_kernel(
                     turns[0] = work.tile([P, HALVES, BANK], F32, name="linear", bufs=2)
                     wrap(0)
                 if n == last + 2:
-                    cos_sin[0] = spare
+                    sin_cos[0] = spare
                     abs_turns(0)
                     sine(0)
                     cosine(0)
@@ -513,17 +519,16 @@ def tile_quantumcoherencelayer_kernel(
                     straight_products(i)
                     if ending:
                         real_mean(i)
-                    cross_product(i, 0)
-                    if not cross_on_vector(i, 1):
-                        cross_product(i, 1)
+                    cross_products(i)
                     if not ending:
                         real_mean(i)
                 if before:
                     imag_mean(i - 1)
-                    fold_real(i - 1)
+                    for h in range(HALVES):
+                        fold_real(i - 1, h)
                     imag_spread(i - 1)
                     for t in trig:
-                        cos_sin[t] = angles.tile([P, 2, D], F32, name="cos_sin")
+                        sin_cos[t] = angles.tile([P, 2, D], F32, name="sin_cos")
                         abs_turns(t)
                     for h in range(HALVES):
                         square_real(i - 1, h)
@@ -537,13 +542,15 @@ def tile_quantumcoherencelayer_kernel(
                     layer_norm_real(i - 2, 0)
                 if 2 <= i + 3 < TILES:
                     multiply(i + 3, sums_banks())
-                if two_before:
+                if two_before and not ending:
                     unfold_real(i - 2, 1)
                 if before:
                     sum_squares(i - 1)
+                if two_before and ending:
+                    unfold_real(i - 2, 1)
                 for t in trig:
                     if not before:
-                        cos_sin[t] = angles.tile([P, 2, D], F32, name="cos_sin")
+                        sin_cos[t] = angles.tile([P, 2, D], F32, name="sin_cos")
                         abs_turns(t)
                     sine(t)
                     cosine(t)
@@ -559,30 +566,31 @@ def tile_quantumcoherencelayer_kernel(
                 if two_before:
                     layer_norm_imag_second(i - 2)
                     layer_norm_real(i - 2, 1)
+                if i == TILES - 1:
+                    fold_real(i, 0)
                 if before:
                     unfold_real(i - 1, 0)
                 if here:
                     combine_imag(i)
 
             last = TILES - 1
-            fold_real(last)
-            square_real(last, 0)
-            square_real(last, 1)
-            sum_squares(last)
+            fold_real(last, 1)
             imag_mean(last)
             imag_spread(last)
-            real_spread(last)
+            for h in range(HALVES):
+                square_real(last, h)
             layer_norm_real(last - 1, 0)
             unfold_real(last - 1, 1)
+            sum_squares(last)
+            layer_norm_imag_second(last - 1)
+            layer_norm_imag_first(last)
+            layer_norm_real(last - 1, 1)
+            real_spread(last)
             mean_squares(last)
             deviations(last)
-            layer_norm_imag_second(last - 1)
-            layer_norm_real(last - 1, 1)
-            layer_norm_imag_first(last)
-            weigh_real(last, 0)
-            weigh_real(last, 1)
-            unfold_real(last, 0)
+            for h in range(HALVES):
+                weigh_real(last, h)
+                unfold_real(last, h)
             layer_norm_imag_second(last)
-            layer_norm_real(last, 0)
-            unfold_real(last, 1)
-            layer_norm_real(last, 1)
+            for h in range(HALVES):
+                layer_norm_real(last, h)

@@ -73,6 +73,7 @@ def tile_quantumcoherencelayer_kernel(
         shift_rows = keep.tile([P, D], BF16)
         identity_bf = keep.tile([P, P], BF16)
         weight_cols = keep.tile([P, BLOCKS * HALVES], F32)
+        odd_turns = keep.tile([P, HALVES, BANK], F32)
         spare = keep.tile([P, 2, D], F32)
 
         nc.vector.memset(one_col[:], 1.0)
@@ -111,10 +112,13 @@ def tile_quantumcoherencelayer_kernel(
             nc.scalar.copy(out=grouped[i][:].bitcast(F32), in_=flipped[i][:].rearrange("p g u r -> p g r u"))
 
         def square(i, piece):
-            if piece == 0:
-                squared[i] = work.tile([P, 2, D], F32, name="squared")
-            cols = slice(D // UNITS * piece, D // UNITS * (piece + 1))
-            nc.scalar.activation(out=squared[i][:, :, cols], in_=x_in[i][:, :, cols], func=ACT.Square)
+            h, quarter = piece // 2, D // UNITS
+            if piece % 2 == 0:
+                squared[i, h] = work.tile([P, 2, BANK], F32, name="squared", bufs=5)
+            nc.scalar.activation(
+                out=squared[i, h][:, :, quarter * (piece % 2) : quarter * (piece % 2 + 1)],
+                in_=x_in[i][:, :, quarter * piece : quarter * (piece + 1)], func=ACT.Square,
+            )
 
         def linear_terms(i):
             linear[i] = work.tile([P, 2, D], F32, name="linear", bufs=2)
@@ -138,11 +142,12 @@ def tile_quantumcoherencelayer_kernel(
         def fold(n):
             i, h, shifted = unit_of(n)
             folded[n] = psum1.tile([P, BANK], F32, name="folded")
-            terms = [squared[i][:, 0, :], squared[i][:, 1, :]]
+            half = slice(BANK * h, BANK * (h + 1))
+            terms = [squared[i, h][:, 0, :], squared[i, h][:, 1, :]]
             if shifted:
-                terms = terms + [linear[i][:, 0, :], linear[i][:, 1, :]]
+                terms = terms + [linear[i][:, 0, half], linear[i][:, 1, half]]
             for block in range(BLOCKS):
-                cols = slice(BANK * h + P * block, BANK * h + P * (block + 1))
+                cols = slice(P * block, P * (block + 1))
                 for t, term in enumerate(terms):
                     nc.tensor.matmul(
                         out=folded[n][:, P * block : P * (block + 1)], lhsT=term[:, cols], rhs=identity[:],
@@ -216,7 +221,7 @@ def tile_quantumcoherencelayer_kernel(
             return turns_early[:, i : i + 1] if i < EARLY_TILES else turns_late[:, i - EARLY_TILES : i - EARLY_TILES + 1]
 
         def on_vector(i, h):
-            return i > 0 and (h == 1 or i % 2 == 1 or i == 2)
+            return i > 0 and (h == 1 or i <= 3)
 
         def add_magic(i, h):
             nc.scalar.activation(
@@ -239,7 +244,10 @@ def tile_quantumcoherencelayer_kernel(
         def whole_turns_on_vector(i):
             for h in range(HALVES):
                 if on_vector(i, h):
-                    by_vector = angles.tile([P, BANK], I32, name="by_vector")
+                    if i == 1:
+                        by_vector = work.tile([P, BANK], I32, name="inverse_t")
+                    else:
+                        by_vector = angles.tile([P, BANK], I32, name="by_vector")
                     rounded[i, h] = by_vector[:]
                     nc.vector.tensor_scalar_mul(out=rounded[i, h], in0=sums[i][h], scalar1=turns_per_unit(i))
 
@@ -473,33 +481,37 @@ def tile_quantumcoherencelayer_kernel(
                     turns_of(nc.vector, slice(0, EARLY_TILES), turns_early)
                 if n == UNITS * EARLY_TILES + 2:
                     turn_weight()
-                if n == last - 3:
+                if n == last - 4:
                     multiply(0, [psum1.tile([P, BANK], F32, name="flipped", bufs=2)[:] for h in range(HALVES)])
-                if n == last - 2:
+                if n == last - 3:
                     early = work.tile([P, HALVES, BANK], F32, name="linear", bufs=2)
                     rounded[0, 0], rounded[0, 1] = early[:, 0, :], early[:, 1, :]
                     add_magic(0, 0)
-                if n == last - 1:
+                if n == last - 2:
                     add_magic(0, 1)
-                if n == last:
+                if n == last - 1:
                     take_magic_away(0, 0)
                     take_magic_away(0, 1)
-                if n == last + 1:
-                    nc.scalar.activation(out=table_warmer[:], in_=one_col[:], func=ACT.Sin)
+                if n == last:
                     turns[0] = work.tile([P, HALVES, BANK], F32, name="linear", bufs=2)
                     wrap(0)
-                if n == last + 2:
+                if n == last + 1:
+                    nc.scalar.activation(out=table_warmer[:], in_=one_col[:], func=ACT.Sin)
                     sin_cos[0] = spare
                     abs_turns(0)
                     sine(0)
                     cosine(0)
+                    multiply(1, [psum1.tile([P, BANK], F32, name="folded")[:] for h in range(HALVES)])
+                if n == last + 2:
+                    turns[1] = odd_turns
+                    wrap(1)
 
         with tc.psum_pool(name="psum", bufs=1) as psum, tc.tile_pool(
             name="angles", bufs=2, reuse_waits="tile"
         ) as angles, tc.tile_pool(name="results", bufs=2, reuse_waits="tile") as results, tc.tile_pool(
             name="small", bufs=4, reuse_waits="tile"
         ) as small, tc.tile_pool(name="turned", bufs=1) as turned:
-            multiply(1, sums_banks())
+            multiply(2, sums_banks())
             gain = psum.tile([P, D], BF16, name="gain")
             shift = psum.tile([P, D], BF16, name="shift")
             for row, repeated in enumerate((gain, shift)):
@@ -508,20 +520,18 @@ def tile_quantumcoherencelayer_kernel(
                     nc.tensor.matmul(
                         out=repeated[:, n_cols], lhsT=ones[:], rhs=gain_shift_rows[:, row, n_cols], start=True, stop=True
                     )
-            nc.scalar.copy(out=shift_rows[:], in_=shift[:])
             turns_of(nc.gpsimd, slice(EARLY_TILES, TILES), turns_late)
 
-            for i in range(-2, TILES):
-                here, before, two_before, ahead = i >= 0, i >= 1, i >= 2, i + 3 < TILES
+            for i in range(TILES):
+                before, two_before, ahead = i >= 1, i >= 2, i + 3 < TILES
                 ending = i >= TILES - 2
-                trig = [t for t in {0: (1, 2), 1: ()}.get(i, (i + 1,)) if 1 <= t < TILES]
-                if here:
-                    straight_products(i)
-                    if ending:
-                        real_mean(i)
-                    cross_products(i)
-                    if not ending:
-                        real_mean(i)
+                trig = [t for t in {0: (1, 2), 1: ()}.get(i, (i + 1,)) if t < TILES]
+                straight_products(i)
+                if ending:
+                    real_mean(i)
+                cross_products(i)
+                if not ending:
+                    real_mean(i)
                 if before:
                     imag_mean(i - 1)
                     for h in range(HALVES):
@@ -533,14 +543,14 @@ def tile_quantumcoherencelayer_kernel(
                     for h in range(HALVES):
                         square_real(i - 1, h)
                         weigh_real(i - 1, h)
-                if 1 <= i + 2 < TILES:
-                    turns[i + 2] = angles.tile([P, HALVES, BANK], F32, name="turns")
+                if i + 2 < TILES:
+                    turns[i + 2] = odd_turns if i % 2 == 1 else angles.tile([P, HALVES, BANK], F32, name="turns", bufs=1)
                     wrap(i + 2)
                 if before:
                     layer_norm_imag_first(i - 1)
                 if two_before:
                     layer_norm_real(i - 2, 0)
-                if 2 <= i + 3 < TILES:
+                if ahead:
                     multiply(i + 3, sums_banks())
                 if two_before and not ending:
                     unfold_real(i - 2, 1)
@@ -554,6 +564,8 @@ def tile_quantumcoherencelayer_kernel(
                         abs_turns(t)
                     sine(t)
                     cosine(t)
+                if i == 0:
+                    nc.scalar.copy(out=shift_rows[:], in_=shift[:])
                 if ahead:
                     rounded_by_scalar(i + 3, 0)
                 if before:
@@ -570,8 +582,7 @@ def tile_quantumcoherencelayer_kernel(
                     fold_real(i, 0)
                 if before:
                     unfold_real(i - 1, 0)
-                if here:
-                    combine_imag(i)
+                combine_imag(i)
 
             last = TILES - 1
             fold_real(last, 1)

import math

import concourse.mybir as mybir
from concourse.masks import make_identity

F32 = mybir.dt.float32
BF16 = mybir.dt.bfloat16
I32 = mybir.dt.int32
U32 = mybir.dt.uint32
U8 = mybir.dt.uint8
FP8X4 = mybir.dt.float8_e4m3fn_x4
ALU = mybir.AluOpType
ACT = mybir.ActivationFunctionType

P = 128
D = 1024
TOKENS = 2048
TILES = TOKENS // P
PACK = 4
K_PASS = P * PACK
PASSES = D // K_PASS
PAIRS_PER_PASS = K_PASS // 2
BANK = 512
HALVES = D // BANK
QUADRANT = 32
SCALE_ROWS = 4
BLOCKS = BANK // P
UNITS = 2 * HALVES
EPS = 1e-8
ROUND_MAGIC = 12582912.0
TWO_PI = 2.0 * math.pi

EARLY_TILES = 12

FLOPS = 2 * TOKENS * D * D


def tile_quantumcoherencelayer_kernel(
    tc, x_real, x_imag, w_words, w_scale_rows, coherence_factor, ln_weight, ln_bias, out_real, out_imag
):
    nc = tc.nc
    by_tile = "(p t) d -> p t d"
    x_dram = (
        x_real.flatten_outer_dims().rearrange(by_tile, t=TILES),
        x_imag.flatten_outer_dims().rearrange(by_tile, t=TILES),
    )
    out_dram = (
        out_real.flatten_outer_dims().rearrange(by_tile, t=TILES),
        out_imag.flatten_outer_dims().rearrange(by_tile, t=TILES),
    )

    with tc.tile_pool(name="keep", bufs=1) as keep, tc.manual_schedule():
        unit = keep.tile([P, TILES, 2, D], F32)
        x_codes = keep.tile([P, TILES, PASSES, P], U32, align_bytes=64)
        x_scales = keep.tile([P, TILES, PASSES, P], U8, align_bytes=64)
        w_codes = keep.tile([P, PASSES, D], U32, align_bytes=64)
        w_scales = keep.tile([P, PASSES, D], U8, align_bytes=64)
        ones = keep.tile([P, P], BF16)
        gain_shift_rows = keep.tile([P, 2, D], BF16)
        factor_bf = keep.tile([P, 1], BF16)
        factor = keep.tile([P, 1], F32)
        identity = keep.tile([P, P], F32)
        one_col = keep.tile([P, 1], F32)
        eps_col = keep.tile([P, 1], F32)
        magic_col = keep.tile([P, 1], F32)
        minus_magic_col = keep.tile([P, 1], F32)
        quarter_turn_col = keep.tile([P, 1], F32)
        table_warmer = keep.tile([P, 1], F32)
        minus_half = keep.tile([P, 2], F32)
        phase_sums = keep.tile([P, 2, HALVES, TILES], F32)
        turns_early = keep.tile([P, EARLY_TILES], F32)
        turns_late = keep.tile([P, TILES - EARLY_TILES], F32)
        shift_rows = keep.tile([P, D], BF16)
        identity_bf = keep.tile([P, P], BF16)
        weight_cols = keep.tile([P, BLOCKS * HALVES], F32)
        odd_turns = keep.tile([P, HALVES, BANK], F32)
        spare = keep.tile([P, 2, D], F32)

        nc.vector.memset(one_col[:], 1.0)
        nc.vector.tensor_scalar_mul(out=eps_col[:], in0=one_col[:], scalar1=EPS)
        nc.vector.tensor_scalar_mul(out=quarter_turn_col[:], in0=one_col[:], scalar1=0.5 * math.pi)
        nc.vector.memset(magic_col[:], ROUND_MAGIC)
        nc.vector.memset(minus_magic_col[:], -ROUND_MAGIC)
        nc.vector.memset(minus_half[:], -0.5)
        nc.vector.memset(ones[:], 1.0)
        nc.vector.memset(gain_shift_rows[:], 0.0)
        nc.vector.memset(w_scales[:].rearrange("p g n -> p (g n)").bitcast(I32), 0)
        make_identity(nc, identity[:])
        nc.vector.tensor_copy(out=identity_bf[:], in_=identity[:])
        nc.scalar.activation(out=table_warmer[:], in_=one_col[:], func=ACT.Abs_reciprocal_sqrt)

        x_in, squared, linear, grouped, folded, inverse_t, unfolded = {}, {}, {}, {}, {}, {}, {}

        def load(i):
            x_in[i] = stream.tile([P, 2, D], BF16, name="x_in")
            for part in range(2):
                nc.sync.dma_start(out=x_in[i][:, part, :], in_=x_dram[part][:, i, :])

        def flip(i):
            pairs = x_in[i][:, 0, :].bitcast(F32)
            flipped[i] = psum1.tile([P, PASSES, 2, P], F32, name="flipped", bufs=2)
            for g in range(PASSES):
                for u in range(2):
                    nc.tensor.transpose(
                        flipped[i][:, g, u, :],
                        pairs[:, PAIRS_PER_PASS * g + u : PAIRS_PER_PASS * (g + 1) : 2],
                        identity[:],
                    )

        def group(i):
            grouped[i] = work.tile([P, PASSES, P, PACK], BF16, name="grouped", align_bytes=64, bufs=2)
            nc.scalar.copy(out=grouped[i][:].bitcast(F32), in_=flipped[i][:].rearrange("p g u r -> p g r u"))

        def square(i, piece):
            h, quarter = piece // 2, D // UNITS
            if piece % 2 == 0:
                squared[i, h] = work.tile([P, 2, BANK], F32, name="squared", bufs=5)
            nc.scalar.activation(
                out=squared[i, h][:, :, quarter * (piece % 2) : quarter * (piece % 2 + 1)],
                in_=x_in[i][:, :, quarter * piece : quarter * (piece + 1)], func=ACT.Square,
            )

        def linear_terms(i):
            linear[i] = work.tile([P, 2, D], F32, name="linear", bufs=2)
            pieces = (slice(0, BANK), slice(BANK, D)) if i == 0 else (slice(0, D),)
            for cols in pieces:
                nc.gpsimd.tensor_scalar(
                    out=linear[i][:, :, cols], in0=x_in[i][:, :, cols], scalar1=2.0 * EPS, scalar2=EPS * EPS,
                    op0=ALU.mult, op1=ALU.add,
                )

        def quantise(i):
            nc.vector.quantize_mx(
                out=x_codes[:, i].rearrange("p g r -> p (g r)").bitcast(FP8X4),
                scales=x_scales[:, i].rearrange("p g r -> p (g r)"),
                in_=grouped[i][:].rearrange("p g r t -> p (g r t)"),
            )

        def unit_of(n):
            return n // UNITS, (n % UNITS) // 2, n % 2 == 1

        def fold(n):
            i, h, shifted = unit_of(n)
            folded[n] = psum1.tile([P, BANK], F32, name="folded")
            half = slice(BANK * h, BANK * (h + 1))
            terms = [squared[i, h][:, 0, :], squared[i, h][:, 1, :]]
            if shifted:
                terms = terms + [linear[i][:, 0, half], linear[i][:, 1, half]]
            for block in range(BLOCKS):
                cols = slice(P * block, P * (block + 1))
                for t, term in enumerate(terms):
                    nc.tensor.matmul(
                        out=folded[n][:, P * block : P * (block + 1)], lhsT=term[:, cols], rhs=identity[:],
                        is_transpose=True, start=(t == 0), stop=(t == len(terms) - 1),
                    )

        def roots(n):
            i, h, shifted = unit_of(n)
            inverse_t[n] = work.tile([P, BANK], F32, name="inverse_t")
            if shifted:
                nc.scalar.activation(out=inverse_t[n][:], in_=folded[n][:], func=ACT.Abs_reciprocal_sqrt)
            else:
                nc.scalar.activation(
                    out=inverse_t[n][:], in_=folded[n][:], func=ACT.Abs_reciprocal_sqrt, bias=eps_col[:]
                )

        def unfold(n):
            unfolded[n] = psum1.tile([P, 1, BANK], F32, name="unfolded")
            for block in range(BLOCKS):
                cols = slice(P * block, P * (block + 1))
                nc.tensor.transpose(unfolded[n][:, 0, cols], inverse_t[n][:, cols], identity[:])

        def products(n):
            i, h, shifted = unit_of(n)
            cols = slice(BANK * h, BANK * (h + 1))
            if shifted:
                for part in range(2):
                    nc.vector.scalar_tensor_tensor(
                        out=shift_rows[:, BANK * part : BANK * (part + 1)], in0=x_in[i][:, part, cols], scalar=EPS, in1=unfolded[n][:, 0, :],
                        op0=ALU.add, op1=ALU.mult, accum_out=phase_sums[:, part, h, i : i + 1],
                    )
            else:
                nc.vector.tensor_tensor(
                    out=unit[:, i, :, cols], in0=x_in[i][:, :, cols],
                    in1=unfolded[n][:].to_broadcast([P, 2, BANK]), op=ALU.mult,
                )

        def prepare(i, step):
            square(i, step)
            if step == 0:
                linear_terms(i)
                flip(i)
            if step == 1:
                group(i)
            if step == 3:
                quantise(i)

        sums, rounded, turns, sin_cos, real, total, minus_mean, spread, inv_std = {}, {}, {}, {}, {}, {}, {}, {}, {}
        real_t, real_t_rows, real_back, squares_t, variance, result, mean_square, minus_real_mean = {}, {}, {}, {}, {}, {}, {}, {}

        def multiply(i, banks):
            sums[i] = banks
            for h in range(HALVES):
                n_cols = slice(BANK * h, BANK * (h + 1))
                for g in range(PASSES):
                    nc.tensor.matmul_mx(
                        out=sums[i][h],
                        lhsT=x_codes[:, i, g, :].bitcast(FP8X4),
                        lhsT_scale=x_scales[:, i, g, :],
                        rhs=w_codes[:, g, n_cols].bitcast(FP8X4),
                        rhs_scale=w_scales[:, g, n_cols],
                        start=(g == 0),
                        stop=(g == PASSES - 1),
                    )

        def sums_banks():
            both = psum.tile([P, HALVES, BANK], F32, name="sums")
            return [both[:, h, :] for h in range(HALVES)]

        def turns_per_unit(i):
            return turns_early[:, i : i + 1] if i < EARLY_TILES else turns_late[:, i - EARLY_TILES : i - EARLY_TILES + 1]

        def on_vector(i, h):
            return i > 0 and (h == 1 or i <= 3)

        def add_magic(i, h):
            nc.scalar.activation(
                out=rounded[i, h], in_=sums[i][h], func=ACT.Identity,
                scale=turns_per_unit(i), bias=magic_col[:],
            )

        def take_magic_away(i, h):
            if on_vector(i, h):
                return
            nc.scalar.activation(out=rounded[i, h], in_=rounded[i, h], func=ACT.Identity, bias=minus_magic_col[:])

        def rounded_by_scalar(i, h):
            if on_vector(i, h):
                return
            by_scalar = angles.tile([P, BANK], F32, name="by_scalar")
            rounded[i, h] = by_scalar[:]
            add_magic(i, h)

        def whole_turns_on_vector(i):
            for h in range(HALVES):
                if on_vector(i, h):
                    if i == 1:
                        by_vector = work.tile([P, BANK], I32, name="inverse_t")
                    else:
                        by_vector = angles.tile([P, BANK], I32, name="by_vector")
                    rounded[i, h] = by_vector[:]
                    nc.vector.tensor_scalar_mul(out=rounded[i, h], in0=sums[i][h], scalar1=turns_per_unit(i))

        def wrap(i):
            whole_turns_on_vector(i)
            for h in range(HALVES):
                nc.vector.scalar_tensor_tensor(
                    out=turns[i][:, h, :], in0=sums[i][h], scalar=turns_per_unit(i),
                    in1=rounded[i, h], op0=ALU.mult, op1=ALU.subtract,
                )

        def abs_turns(i):
            nc.scalar.activation(out=sin_cos[i][:, 1, :], in_=turns[i][:].rearrange("p h w -> p (h w)"), func=ACT.Abs)

        def sine(i):
            nc.scalar.activation(
                out=sin_cos[i][:, 0, :], in_=turns[i][:].rearrange("p h w -> p (h w)"), func=ACT.Sin, scale=TWO_PI
            )

        def cosine(i):
            nc.scalar.activation(
                out=sin_cos[i][:, 1, :], in_=sin_cos[i][:, 1, :], func=ACT.Sin, scale=-TWO_PI, bias=quarter_turn_col[:]
            )

        def straight_products(i):
            real[i] = spare if i % 2 == 1 else results.tile([P, 2, D], F32, name="real", bufs=1)
            total[i] = small.tile([P, 3], F32, name="total")
            for part in (1, 0) if b_cos_on_vector(i) else (0, 1):
                nc.vector.scalar_tensor_tensor(
                    out=real[i][:, part, :], in0=unit[:, i, part, :], scalar=(1.0, -1.0)[part],
                    in1=sin_cos[i][:, 1 - part, :], op0=ALU.mult, op1=ALU.mult, accum_out=total[i][:, part : part + 1],
                )
                if part == 1 and b_cos_on_vector(i):
                    b_cos(i)

        def fold_real(i, h):
            if h == 0:
                real_t[i] = psum.tile([P, HALVES, BANK], F32, name="real_t")
            for block in range(BLOCKS):
                cols = slice(BANK * h + P * block, BANK * h + P * (block + 1))
                terms = (real[i][:, 0, cols], real[i][:, 1, cols], minus_real_mean[i][:].to_broadcast([P, P]))
                for t, term in enumerate(terms):
                    nc.tensor.matmul(
                        out=real_t[i][:, h, P * block : P * (block + 1)], lhsT=term,
                        rhs=identity[:], is_transpose=True, start=(t == 0), stop=(t == len(terms) - 1),
                    )

        def square_real(i, h):
            if h == 0:
                squares_t[i] = turned.tile([P, HALVES, BANK], F32, name="squares_t", bufs=1)
            nc.scalar.activation(out=squares_t[i][:, h, :], in_=real_t[i][:, h, :], func=ACT.Square, scale=float(D))

        def weigh_real(i, h):
            if h == 0:
                real_t_rows[i] = turned.tile([P, HALVES, BANK], F32, name="real_t_rows", bufs=2)
            for block in range(BLOCKS):
                cols = slice(P * block, P * (block + 1))
                nc.scalar.activation(
                    out=real_t_rows[i][:, h, cols], in_=real_t[i][:, h, cols], func=ACT.Copy,
                    scale=weight_cols[:, BLOCKS * h + block : BLOCKS * h + block + 1],
                )

        def sum_squares(i):
            variance[i] = psum.tile([P, BANK], F32, name="variance")
            for h in range(HALVES):
                for block in range(BLOCKS):
                    nc.tensor.matmul(
                        out=variance[i][:, 0:P], lhsT=squares_t[i][:, h, P * block : P * (block + 1)], rhs=identity[:],
                        is_transpose=True, start=(h == 0 and block == 0), stop=(h == HALVES - 1 and block == BLOCKS - 1),
                    )

        def unfold_real(i, h):
            if i == TILES - 1 and h == 1:
                real_back[i, h] = psum.tile([P, BANK], F32, name="variance")
            else:
                real_back[i, h] = psum.tile([P, BANK], F32, name="real_back")
            for block in range(BLOCKS):
                cols = slice(P * block, P * (block + 1))
                nc.tensor.transpose(real_back[i, h][:, cols], real_t_rows[i][:, h, cols], identity[:])

        def b_cos_on_vector(i):
            return i in (0, 1, TILES - 2, TILES - 1)

        def b_cos(i):
            nc.vector.tensor_tensor(out=unit[:, i, 1, :], in0=unit[:, i, 1, :], in1=sin_cos[i][:, 1, :], op=ALU.mult)

        def cross_products(i):
            parts = slice(0, 1) if b_cos_on_vector(i) else slice(0, 2)
            nc.gpsimd.tensor_tensor(
                out=unit[:, i, parts, :], in0=unit[:, i, parts, :], in1=sin_cos[i][:, parts, :], op=ALU.mult
            )

        def combine_imag(i):
            nc.vector.scalar_tensor_tensor(
                out=unit[:, i, 0, :], in0=unit[:, i, 0, :], scalar=1.0, in1=unit[:, i, 1, :],
                op0=ALU.mult, op1=ALU.add, accum_out=total[i][:, 2:3],
            )

        def real_mean(i):
            minus_real_mean[i] = small.tile([P, 1], F32, name="minus_real_mean")
            nc.gpsimd.tensor_scalar(
                out=minus_real_mean[i][:], in0=total[i][:, 0:1], scalar1=total[i][:, 1:2], scalar2=-1.0 / D,
                op0=ALU.add, op1=ALU.mult,
            )

        def imag_mean(i):
            minus_mean[i] = small.tile([P, 1], F32, name="minus_mean")
            nc.scalar.activation(out=minus_mean[i][:], in_=total[i][:, 2:3], func=ACT.Copy, scale=-1.0 / D)

        def imag_spread(i):
            unread = small.tile([P, D], BF16, name="unread", bufs=1)
            spread[i] = small.tile([P, 2], F32, name="spread")
            nc.scalar.activation(
                out=unread[:], in_=unit[:, i, 0, :], func=ACT.Square, scale=-float(D), bias=total[i][:, 2:3],
                accum_out=spread[i][:, 1:2],
            )

        def real_spread(i):
            unread = small.tile([P, P], BF16, name="unread_sum", bufs=1)
            nc.scalar.activation(
                out=unread[:], in_=variance[i][:, 0:P], func=ACT.Identity, accum_out=spread[i][:, 0:1]
            )

        def mean_squares(i):
            mean_square[i] = small.tile([P, 2], F32, name="mean_square")
            nc.scalar.activation(
                out=mean_square[i][:], in_=spread[i][:], func=ACT.Identity, scale=1.0 / D**3, bias=eps_col[:]
            )

        def deviations(i):
            inv_std[i] = small.tile([P, 2], F32, name="inv_std")
            nc.gpsimd.tensor_tensor(out=inv_std[i][:], in0=mean_square[i][:], in1=minus_half[:], op=ALU.pow)

        def layer_norm_real(i, h):
            if h == 0:
                result[i] = results.tile([P, D], F32, name="result", bufs=2)
            cols = slice(BANK * h, BANK * (h + 1))
            nc.vector.scalar_tensor_tensor(
                out=result[i][:, cols], in0=real_back[i, h][:], scalar=inv_std[i][:, 0:1], in1=shift_rows[:, cols],
                op0=ALU.mult, op1=ALU.add,
            )
            if i == TILES - 1:
                nc.sync.dma_start(out=out_dram[0][:, i, cols], in_=result[i][:, cols])
            elif h == HALVES - 1:
                nc.sync.dma_start(out=out_dram[0][:, i, :], in_=result[i][:])

        def layer_norm_imag_first(i):
            nc.vector.scalar_tensor_tensor(
                out=unit[:, i, 0, :], in0=unit[:, i, 0, :], scalar=minus_mean[i][:], in1=gain[:],
                op0=ALU.add, op1=ALU.mult,
            )

        def layer_norm_imag_second(i):
            values = unit[:, i, 0, :]
            nc.vector.scalar_tensor_tensor(
                out=values, in0=values, scalar=inv_std[i][:, 1:2], in1=shift[:], op0=ALU.mult, op1=ALU.add
            )
            nc.sync.dma_start(out=out_dram[1][:, i, :], in_=values)

        def turns_of(engine, tiles, turns_column):
            whole_sums = phase_sums[:, :, 0, tiles]
            engine.tensor_tensor(out=whole_sums, in0=whole_sums, in1=phase_sums[:, :, 1, tiles], op=ALU.add)
            engine.tensor_tensor(out=whole_sums, in0=whole_sums, in1=whole_sums, op=ALU.mult)
            engine.tensor_tensor(
                out=turns_column[:], in0=phase_sums[:, 0, 0, tiles], in1=phase_sums[:, 1, 0, tiles], op=ALU.add
            )
            engine.tensor_scalar(
                out=turns_column[:], in0=turns_column[:], scalar1=-1.0 / (D * D), scalar2=1.0, op0=ALU.mult, op1=ALU.add
            )
            engine.tensor_scalar(
                out=turns_column[:], in0=turns_column[:], scalar1=factor[:], scalar2=1.0 / TWO_PI,
                op0=ALU.mult, op1=ALU.mult,
            )

        def load_the_rest():
            nc.sync.dma_start(out=factor_bf[:], in_=coherence_factor.partition_broadcast(P))
            for g in range(PASSES):
                nc.sync.dma_start(
                    out=w_codes[:, g, :].bitcast(I32), in_=w_words[g].rearrange("p n t -> p (n t)").bitcast(I32)
                )
            for quadrant in range(P // QUADRANT):
                rows = slice(SCALE_ROWS * quadrant, SCALE_ROWS * (quadrant + 1))
                nc.sync.dma_start(
                    out=w_scales[QUADRANT * quadrant : QUADRANT * quadrant + SCALE_ROWS, :, :].bitcast(I32),
                    in_=w_scale_rows[:, rows, :].rearrange("g r n -> r g n").bitcast(I32),
                )
            nc.sync.dma_start(out=gain_shift_rows[0:1, 0, :], in_=ln_weight.unsqueeze(0))
            nc.sync.dma_start(out=gain_shift_rows[0:1, 1, :], in_=ln_bias.unsqueeze(0))

        def turn_weight():
            weight_t = psum1.tile([P, BLOCKS * HALVES, P], BF16, name="flipped", bufs=2)
            for block in range(BLOCKS * HALVES):
                nc.tensor.transpose(
                    weight_t[:, block, :], gain_shift_rows[:, 0, P * block : P * (block + 1)], identity_bf[:]
                )
            nc.vector.tensor_copy(out=weight_cols[:], in_=weight_t[:, :, 0])

        flipped = {}
        last = UNITS * TILES - 1
        with tc.tile_pool(name="stream", bufs=4) as stream, tc.tile_pool(name="work", bufs=3) as work, tc.psum_pool(
            name="psum1", bufs=3
        ) as psum1:
            for i in range(3):
                load(i)
            for piece in range(UNITS):
                square(0, piece)
            linear_terms(0)
            flip(0)
            for n in range(UNITS * TILES + 3):
                i, step = n // UNITS, n % UNITS
                if n < UNITS * TILES:
                    fold(n)
                if 1 <= n <= UNITS * TILES:
                    roots(n - 1)
                if n == 1:
                    group(0)
                if i + 1 < TILES:
                    prepare(i + 1, step)
                if n == 2:
                    quantise(0)
                if 2 <= n <= UNITS * TILES + 1:
                    unfold(n - 2)
                if n >= 3:
                    products(n - 3)
                if step == 3 and i + 3 < TILES:
                    load(i + 3)
                if n == 11:
                    load_the_rest()
                if n == UNITS * (EARLY_TILES + 1) + 2:
                    nc.vector.tensor_copy(out=factor[:], in_=factor_bf[:])
                    turns_of(nc.vector, slice(0, EARLY_TILES), turns_early)
                if n == UNITS * EARLY_TILES + 2:
                    turn_weight()
                if n == last - 4:
                    multiply(0, [psum1.tile([P, BANK], F32, name="flipped", bufs=2)[:] for h in range(HALVES)])
                if n == last - 3:
                    early = work.tile([P, HALVES, BANK], F32, name="linear", bufs=2)
                    rounded[0, 0], rounded[0, 1] = early[:, 0, :], early[:, 1, :]
                    add_magic(0, 0)
                if n == last - 2:
                    add_magic(0, 1)
                if n == last - 1:
                    take_magic_away(0, 0)
                    take_magic_away(0, 1)
                if n == last:
                    turns[0] = work.tile([P, HALVES, BANK], F32, name="linear", bufs=2)
                    wrap(0)
                if n == last + 1:
                    nc.scalar.activation(out=table_warmer[:], in_=one_col[:], func=ACT.Sin)
                    sin_cos[0] = spare
                    abs_turns(0)
                    sine(0)
                    cosine(0)
                    multiply(1, [psum1.tile([P, BANK], F32, name="folded")[:] for h in range(HALVES)])
                if n == last + 2:
                    turns[1] = odd_turns
                    wrap(1)

        with tc.psum_pool(name="psum", bufs=1) as psum, tc.tile_pool(
            name="angles", bufs=2, reuse_waits="tile"
        ) as angles, tc.tile_pool(name="results", bufs=2, reuse_waits="tile") as results, tc.tile_pool(
            name="small", bufs=4, reuse_waits="tile"
        ) as small, tc.tile_pool(name="turned", bufs=1) as turned:
            multiply(2, sums_banks())
            gain = psum.tile([P, D], BF16, name="gain")
            shift = psum.tile([P, D], BF16, name="shift")
            for row, repeated in enumerate((gain, shift)):
                for h in range(HALVES):
                    n_cols = slice(BANK * h, BANK * (h + 1))
                    nc.tensor.matmul(
                        out=repeated[:, n_cols], lhsT=ones[:], rhs=gain_shift_rows[:, row, n_cols], start=True, stop=True
                    )
            turns_of(nc.gpsimd, slice(EARLY_TILES, TILES), turns_late)

            for i in range(TILES):
                before, two_before, ahead = i >= 1, i >= 2, i + 3 < TILES
                ending = i >= TILES - 2
                trig = [t for t in {0: (1, 2), 1: ()}.get(i, (i + 1,)) if t < TILES]
                straight_products(i)
                if ending:
                    real_mean(i)
                cross_products(i)
                if not ending:
                    real_mean(i)
                if before:
                    imag_mean(i - 1)
                    for h in range(HALVES):
                        fold_real(i - 1, h)
                    imag_spread(i - 1)
                    for t in trig:
                        sin_cos[t] = angles.tile([P, 2, D], F32, name="sin_cos")
                        abs_turns(t)
                    for h in range(HALVES):
                        square_real(i - 1, h)
                        weigh_real(i - 1, h)
                if i + 2 < TILES:
                    turns[i + 2] = odd_turns if i % 2 == 1 else angles.tile([P, HALVES, BANK], F32, name="turns", bufs=1)
                    wrap(i + 2)
                if before:
                    layer_norm_imag_first(i - 1)
                if two_before:
                    layer_norm_real(i - 2, 0)
                if ahead:
                    multiply(i + 3, sums_banks())
                if two_before and not ending:
                    unfold_real(i - 2, 1)
                if before:
                    sum_squares(i - 1)
                if two_before and ending:
                    unfold_real(i - 2, 1)
                for t in trig:
                    if not before:
                        sin_cos[t] = angles.tile([P, 2, D], F32, name="sin_cos")
                        abs_turns(t)
                    sine(t)
                    cosine(t)
                if i == 0:
                    nc.scalar.copy(out=shift_rows[:], in_=shift[:])
                if ahead:
                    rounded_by_scalar(i + 3, 0)
                if before:
                    real_spread(i - 1)
                if ahead:
                    take_magic_away(i + 3, 0)
                if before:
                    mean_squares(i - 1)
                    deviations(i - 1)
                if two_before:
                    layer_norm_imag_second(i - 2)
                    layer_norm_real(i - 2, 1)
                if i == TILES - 1:
                    fold_real(i, 0)
                if before:
                    unfold_real(i - 1, 0)
                combine_imag(i)

            last = TILES - 1
            fold_real(last, 1)
            imag_mean(last)
            imag_spread(last)
            for h in range(HALVES):
                square_real(last, h)
            layer_norm_real(last - 1, 0)
            unfold_real(last - 1, 1)
            sum_squares(last)
            layer_norm_imag_second(last - 1)
            layer_norm_imag_first(last)
            layer_norm_real(last - 1, 1)
            real_spread(last)
            mean_squares(last)
            deviations(last)
            for h in range(HALVES):
                weigh_real(last, h)
                unfold_real(last, h)
            layer_norm_imag_second(last)
            for h in range(HALVES):
                layer_norm_real(last, h)
